import numpy as np
import ml_dtypes


def mxq(x, axis, fmt="e4m3"):
    dtype, down = {"e4m3": (ml_dtypes.float8_e4m3fn, 7), "e5m2": (ml_dtypes.float8_e5m2, 14)}[fmt]
    v = np.moveaxis(np.asarray(x, np.float32).astype(ml_dtypes.bfloat16).astype(np.float64), axis, -1)
    blocks = v.reshape(v.shape[:-1] + (-1, 32))
    amax = np.abs(blocks).max(-1, keepdims=True)
    byte = np.maximum(np.where(amax > 0, np.frexp(amax)[1] - 1 + 127, 0) - down, 1)
    scale = np.exp2(byte - 127.0)
    codes = (blocks / scale).astype(np.float32).astype(dtype).astype(np.float64)
    return np.moveaxis((codes * scale).reshape(v.shape), -1, axis)


WIDE = False


def mx_kscale(k):
    if not WIDE:
        return np.ones(k)
    levels = np.array([10, -10, 5, -5, 0])
    a = np.random.permutation(np.resize(levels, k // 512 * 4)).reshape(k // 512, 4)
    idx = np.arange(k)
    return np.exp2(a[idx // 512, idx % 128 // 32])


BF16 = ml_dtypes.bfloat16


def bf(x):
    return np.asarray(x, np.float32).astype(BF16)


def f64(x):
    return np.asarray(x).astype(np.float64)


B, EMBED, DETER, STOC, HID, ACT = 512, 1536, 1024, 64, 1024, 12
EPS_LN = 1e-3


def sigmoid(v):
    return 1.0 / (1.0 + np.exp(-v))


def ln(v, g, b):
    m = v.mean(-1, keepdims=True)
    var = ((v - m) ** 2).mean(-1, keepdims=True)
    return (v - m) / np.sqrt(var + EPS_LN) * g + b


def setup_inputs():
    s = mx_kscale(HID)
    r = np.random.standard_normal
    return {
        "x_pre": bf(np.maximum(r((B, HID)), 0.0) * s),
        "deter": bf(r((B, DETER))),
        "mask": bf(np.random.random((B, 1)) < 0.75),
        "w_ih": bf(r((3 * DETER, HID)) * 0.1 / np.sqrt(HID) / s),
        "w_hh": bf(r((3 * DETER, DETER)) * 0.1 / np.sqrt(DETER)),
        "ln_r_g": bf(1.0 + 0.2 * r(DETER)), "ln_r_b": bf(0.2 * r(DETER)),
        "ln_u_g": bf(1.0 + 0.2 * r(DETER)), "ln_u_b": bf(0.2 * r(DETER)),
        "ln_n_g": bf(1.0 + 0.2 * r(DETER)), "ln_n_b": bf(0.2 * r(DETER)),
    }


def reference(x_pre, deter, mask, w_ih, w_hh, ln_r_g, ln_r_b, ln_u_g, ln_u_b, ln_n_g, ln_n_b):
    d = f64(deter) * f64(mask)
    gi = mxq(f64(x_pre), 1, "e4m3") @ mxq(f64(w_ih), 1, "e4m3").T
    gh = mxq(d, 1, "e4m3") @ mxq(f64(w_hh), 1, "e4m3").T
    ri, ui, ni = np.split(gi, 3, axis=1)
    rh, uh, nh = np.split(gh, 3, axis=1)
    reset = sigmoid(ln(ri + rh, f64(ln_r_g), f64(ln_r_b)))
    update = sigmoid(ln(ui + uh, f64(ln_u_g), f64(ln_u_b)))
    newval = np.tanh(ln(ni + reset * nh, f64(ln_n_g), f64(ln_n_b)))
    return update * newval + (1.0 - update) * d

@@ -1,0 +1,229 @@
+from contextlib import ExitStack
+
+import concourse.mybir as mybir
+from concourse.masks import make_identity
+
+F32 = mybir.dt.float32
+BF16 = mybir.dt.bfloat16
+U32 = mybir.dt.uint32
+U8 = mybir.dt.uint8
+FP8X4 = mybir.dt.float8_e4m3fn_x4
+ALU = mybir.AluOpType
+ACT = mybir.ActivationFunctionType
+
+P = 128
+BATCH = 512
+K = 1024
+WIDTH = 1024
+CHUNK = 512
+BLOCKS = CHUNK // P
+PASSES = K // 512
+ROW_TILES = BATCH // P
+HALVES = WIDTH // CHUNK
+EPS_LN = 1e-3
+GATE_R, GATE_U, GATE_N = 0, 1, 2
+
+FLOPS = 2 * 2 * BATCH * K * 3 * WIDTH
+
+
+def quantise_chunk(nc, pools, ident, blocks, codes, scales, vector_helps):
+    grouped = pools["grouped"].tile([P, 4 * PASSES * CHUNK], BF16, align_bytes=64, name="grouped")
+    grouped_words = grouped[:].bitcast(F32).rearrange("p (g c u) -> p g c u", g=PASSES, u=2)
+    for t, block in enumerate(blocks):
+        words = block.bitcast(F32)
+        bank = pools["turned"].tile([P, CHUNK], F32, name="bank")
+        for a in range(2 * PASSES):
+            nc.tensor.transpose(
+                out=bank[:, a * P : (a + 1) * P], in_=words[:, a * P : (a + 1) * P], identity=ident[:]
+            )
+        turned = bank[:].rearrange("p (g u c) -> p g c u", g=PASSES, u=2)
+        if vector_helps and t % 2 == 1:
+            nc.vector.tensor_copy(out=grouped_words[:, :, t * P : (t + 1) * P, :], in_=turned)
+        else:
+            nc.scalar.copy(out=grouped_words[:, :, t * P : (t + 1) * P, :], in_=turned)
+    nc.vector.quantize_mx(out=codes[:].bitcast(FP8X4), scales=scales[:], in_=grouped[:])
+
+
+def load_blocks(nc, pools, rows):
+    blocks = []
+    for t in range(BLOCKS):
+        raw = pools["raw"].tile([P, K], BF16, name="raw")
+        nc.sync.dma_start(out=raw[:], in_=rows[t * P : (t + 1) * P, :])
+        blocks.append(raw[:])
+    return blocks
+
+
+def mx_passes(nc, acc, act, wts, m, first, last):
+    act_codes, act_scales = act
+    wts_codes, wts_scales = wts
+    for g in range(PASSES):
+        rows = slice(g * CHUNK + m * P, g * CHUNK + (m + 1) * P)
+        cols = slice(g * CHUNK, (g + 1) * CHUNK)
+        nc.tensor.matmul_mx(
+            out=acc[:],
+            lhsT=act_codes[:, rows].bitcast(FP8X4),
+            lhsT_scale=act_scales[:, rows],
+            rhs=wts_codes[:, cols].bitcast(FP8X4),
+            rhs_scale=wts_scales[:, cols],
+            start=(first and g == 0),
+            stop=(last and g == PASSES - 1),
+        )
+
+
+def layer_norm_act(nc, pools, neg_half, v, half_sums, gain, bias, func, result):
+    small = pools["small"]
+    scaled_sums = small.tile([P, HALVES], F32, name="scaled_sums")
+    neg_mean = small.tile([P, 1], F32, name="neg_mean")
+    nc.scalar.activation(
+        out=scaled_sums[:], in_=half_sums[:], func=ACT.Identity, scale=-1.0 / WIDTH, accum_out=neg_mean[:]
+    )
+    squares = pools["squares"].tile([P, WIDTH], BF16, name="squares")
+    sum_sq = small.tile([P, 1], F32, name="sum_sq")
+    nc.scalar.activation(out=squares[:], in_=v[:], func=ACT.Square, bias=neg_mean[:], accum_out=sum_sq[:])
+    var_eps = small.tile([P, 1], F32, name="var_eps")
+    nc.gpsimd.tensor_scalar(
+        out=var_eps[:], in0=sum_sq[:], scalar1=1.0 / WIDTH, scalar2=EPS_LN, op0=ALU.mult, op1=ALU.add
+    )
+    rstd = small.tile([P, 1], F32, name="rstd")
+    nc.gpsimd.tensor_tensor(out=rstd[:], in0=var_eps[:], in1=neg_half[:], op=ALU.pow)
+    z = pools["z"].tile([P, WIDTH], F32, name="z")
+    nc.vector.scalar_tensor_tensor(out=z[:], in0=v[:], scalar=neg_mean[:], in1=gain[:], op0=ALU.add, op1=ALU.mult)
+    nc.vector.scalar_tensor_tensor(out=z[:], in0=z[:], scalar=rstd[:], in1=bias[:], op0=ALU.mult, op1=ALU.add)
+    nc.scalar.activation(out=result[:], in_=z[:], func=func)
+
+
+def tile_rssmcell_pa_kernel(
+    tc, x_pre, deter, mask, w_ih, w_hh, ln_r_g, ln_r_b, ln_u_g, ln_u_b, ln_n_g, ln_n_b, out
+):
+    nc = tc.nc
+    with ExitStack() as ctx:
+        pools = {
+            "const": ctx.enter_context(tc.tile_pool(name="const", bufs=1)),
+            "raw": ctx.enter_context(tc.tile_pool(name="raw", bufs=16)),
+            "grouped": ctx.enter_context(tc.tile_pool(name="grouped", bufs=3)),
+            "wts": ctx.enter_context(tc.tile_pool(name="wts", bufs=6)),
+            "gate": ctx.enter_context(tc.tile_pool(name="gate", bufs=ROW_TILES)),
+            "z": ctx.enter_context(tc.tile_pool(name="z", bufs=3)),
+            "squares": ctx.enter_context(tc.tile_pool(name="squares", bufs=2)),
+            "small": ctx.enter_context(tc.tile_pool(name="small", bufs=8)),
+            "turned": ctx.enter_context(tc.psum_pool(name="turned", bufs=4)),
+            "acc": ctx.enter_context(tc.psum_pool(name="acc", bufs=4)),
+        }
+        const = pools["const"]
+
+        ident = const.tile([P, P], F32, name="ident")
+        make_identity(nc, ident[:])
+        ident_bf = const.tile([P, P], BF16, name="ident_bf")
+        make_identity(nc, ident_bf[:])
+        neg_half = const.tile([P, 1], F32, name="neg_half")
+        nc.gpsimd.memset(neg_half[:], -0.5)
+
+        mask_sb = const.tile([P, ROW_TILES], BF16, name="mask_sb")
+        with nc.allow_non_contiguous_dma(reason="512 mask values, one to a partition for each row tile"):
+            nc.scalar.dma_start(out=mask_sb[:], in_=mask.rearrange("(m p) o -> p (m o)", p=P))
+        ln_vectors = [ln_r_g, ln_r_b, ln_u_g, ln_u_b, ln_n_g, ln_n_b]
+        ln_rows = const.tile([P, WIDTH], BF16, name="ln_rows")
+        nc.vector.memset(ln_rows[:], 0.0)
+        for r, vector in enumerate(ln_vectors):
+            nc.scalar.dma_start(out=ln_rows[r : r + 1, :], in_=vector.unsqueeze(0))
+
+        x_codes = const.tile([P, PASSES * CHUNK], U32, align_bytes=64, name="x_codes")
+        x_scales = const.tile([P, PASSES * CHUNK], U8, align_bytes=64, name="x_scales")
+        quantise_chunk(nc, pools, ident, load_blocks(nc, pools, x_pre), x_codes, x_scales, True)
+        d_sb = const.tile([P, ROW_TILES, K], BF16, name="d_sb")
+        for m, raw in enumerate(load_blocks(nc, pools, deter)):
+            nc.vector.tensor_scalar_mul(out=d_sb[:, m, :], in0=raw, scalar1=mask_sb[:, m : m + 1])
+        d_codes = const.tile([P, PASSES * CHUNK], U32, align_bytes=64, name="d_codes")
+        d_scales = const.tile([P, PASSES * CHUNK], U8, align_bytes=64, name="d_scales")
+        quantise_chunk(nc, pools, ident, [d_sb[:, m, :] for m in range(ROW_TILES)], d_codes, d_scales, True)
+        acts = {"ih": (x_codes, x_scales), "hh": (d_codes, d_scales)}
+        weights = {"ih": w_ih, "hh": w_hh}
+
+        def weight_chunk(which, gate, h, vector_helps):
+            first_row = gate * WIDTH + h * CHUNK
+            codes = pools["wts"].tile([P, PASSES * CHUNK], U32, align_bytes=64, name="w_codes")
+            scales = pools["wts"].tile([P, PASSES * CHUNK], U8, align_bytes=64, name="w_scales")
+            blocks = load_blocks(nc, pools, weights[which][first_row : first_row + CHUNK, :])
+            quantise_chunk(nc, pools, ident, blocks, codes, scales, vector_helps)
+            return codes, scales
+
+        def spread(r):
+            bank = pools["turned"].tile([P, WIDTH], BF16, name="bank")
+            for h in range(HALVES):
+                cols = slice(h * CHUNK, (h + 1) * CHUNK)
+                nc.tensor.matmul(
+                    out=bank[:, cols],
+                    lhsT=ident_bf[:, r : r + 1].to_broadcast([P, P]),
+                    rhs=ln_rows[:, cols],
+                    start=True,
+                    stop=True,
+                )
+            everywhere = const.tile([P, WIDTH], BF16, name="ln_spread_%d" % r)
+            nc.vector.tensor_copy(out=everywhere[:], in_=bank[:])
+            return everywhere
+
+        def summed_gate(wts, name):
+            sums = [pools["gate"].tile([P, WIDTH], F32, name=name) for m in range(ROW_TILES)]
+            half_sums = [pools["small"].tile([P, HALVES], F32, name="half_sums") for m in range(ROW_TILES)]
+            for h in range(HALVES):
+                banks = [pools["acc"].tile([P, CHUNK], F32, name="acc") for m in range(ROW_TILES)]
+                for which in ("ih", "hh"):
+                    for m in range(ROW_TILES):
+                        mx_passes(nc, banks[m], acts[which], wts[(which, h)], m, which == "ih", which == "hh")
+                for m in range(ROW_TILES):
+                    nc.scalar.activation(
+                        out=sums[m][:, h * CHUNK : (h + 1) * CHUNK],
+                        in_=banks[m][:],
+                        func=ACT.Identity,
+                        accum_out=half_sums[m][:, h : h + 1],
+                    )
+            return sums, half_sums
+
+        r_gain, r_bias, u_gain, u_bias, n_gain, n_bias = [spread(r) for r in range(len(ln_vectors))]
+
+        summed_order = [("ih", 0), ("hh", 0), ("ih", 1), ("hh", 1)]
+        candidate_order = [("hh", 0), ("ih", 0), ("hh", 1), ("ih", 1)]
+
+        wts = {}
+        for which, h in summed_order:
+            wts[(which, h)] = weight_chunk(which, GATE_R, h, True)
+        reset, half_sums = summed_gate(wts, "r_gate")
+        wts = {}
+        for m in range(ROW_TILES):
+            which, h = candidate_order[m]
+            wts[(which, h)] = weight_chunk(which, GATE_N, h, False)
+            layer_norm_act(nc, pools, neg_half, reset[m], half_sums[m], r_gain, r_bias, ACT.Sigmoid, reset[m])
+
+        blend = [pools["gate"].tile([P, WIDTH], F32, name="n_gate") for m in range(ROW_TILES)]
+        pre_sums = [pools["small"].tile([P, HALVES], F32, name="pre_sums") for m in range(ROW_TILES)]
+        for h in range(HALVES):
+            cols = slice(h * CHUNK, (h + 1) * CHUNK)
+            for m in range(ROW_TILES):
+                acc = pools["acc"].tile([P, CHUNK], F32, name="acc")
+                mx_passes(nc, acc, acts["hh"], wts[("hh", h)], m, True, True)
+                nc.vector.tensor_tensor(out=blend[m][:, cols], in0=reset[m][:, cols], in1=acc[:], op=ALU.mult)
+            for m in range(ROW_TILES):
+                acc = pools["acc"].tile([P, CHUNK], F32, name="acc")
+                mx_passes(nc, acc, acts["ih"], wts[("ih", h)], m, True, True)
+                nc.vector.scalar_tensor_tensor(
+                    out=blend[m][:, cols],
+                    in0=blend[m][:, cols],
+                    scalar=1.0,
+                    in1=acc[:],
+                    op0=ALU.mult,
+                    op1=ALU.add,
+                    accum_out=pre_sums[m][:, h : h + 1],
+                )
+        wts = {}
+        for m in range(ROW_TILES):
+            which, h = summed_order[m]
+            wts[(which, h)] = weight_chunk(which, GATE_U, h, False)
+            layer_norm_act(nc, pools, neg_half, blend[m], pre_sums[m], n_gain, n_bias, ACT.Tanh, blend[m])
+            nc.vector.tensor_tensor(out=blend[m][:], in0=blend[m][:], in1=d_sb[:, m, :], op=ALU.subtract)
+
+        update, half_sums = summed_gate(wts, "u_gate")
+        for m in range(ROW_TILES):
+            layer_norm_act(nc, pools, neg_half, update[m], half_sums[m], u_gain, u_bias, ACT.Sigmoid, update[m])
+            nc.vector.tensor_tensor(out=blend[m][:], in0=blend[m][:], in1=update[m][:], op=ALU.mult)
+            nc.vector.tensor_tensor(out=blend[m][:], in0=blend[m][:], in1=d_sb[:, m, :], op=ALU.add)
+            nc.sync.dma_start(out=out[m * P : (m + 1) * P, :], in_=blend[m][:])

@@ -21,75 +21,10 @@ PASSES = K // 512
 ROW_TILES = BATCH // P
 HALVES = WIDTH // CHUNK
 EPS_LN = 1e-3
-GATE_R, GATE_U, GATE_N = 0, 1, 2
+LOAD_AHEAD = 3
+VECTOR_HELPS_BEFORE = 8
 
 FLOPS = 2 * 2 * BATCH * K * 3 * WIDTH
-
-
-def quantise_chunk(nc, pools, ident, blocks, codes, scales, vector_helps):
-    grouped = pools["grouped"].tile([P, 4 * PASSES * CHUNK], BF16, align_bytes=64, name="grouped")
-    grouped_words = grouped[:].bitcast(F32).rearrange("p (g c u) -> p g c u", g=PASSES, u=2)
-    for t, block in enumerate(blocks):
-        words = block.bitcast(F32)
-        bank = pools["turned"].tile([P, CHUNK], F32, name="bank")
-        for a in range(2 * PASSES):
-            nc.tensor.transpose(
-                out=bank[:, a * P : (a + 1) * P], in_=words[:, a * P : (a + 1) * P], identity=ident[:]
-            )
-        turned = bank[:].rearrange("p (g u c) -> p g c u", g=PASSES, u=2)
-        if vector_helps and t % 2 == 1:
-            nc.vector.tensor_copy(out=grouped_words[:, :, t * P : (t + 1) * P, :], in_=turned)
-        else:
-            nc.scalar.copy(out=grouped_words[:, :, t * P : (t + 1) * P, :], in_=turned)
-    nc.vector.quantize_mx(out=codes[:].bitcast(FP8X4), scales=scales[:], in_=grouped[:])
-
-
-def load_blocks(nc, pools, rows):
-    blocks = []
-    for t in range(BLOCKS):
-        raw = pools["raw"].tile([P, K], BF16, name="raw")
-        nc.sync.dma_start(out=raw[:], in_=rows[t * P : (t + 1) * P, :])
-        blocks.append(raw[:])
-    return blocks
-
-
-def mx_passes(nc, acc, act, wts, m, first, last):
-    act_codes, act_scales = act
-    wts_codes, wts_scales = wts
-    for g in range(PASSES):
-        rows = slice(g * CHUNK + m * P, g * CHUNK + (m + 1) * P)
-        cols = slice(g * CHUNK, (g + 1) * CHUNK)
-        nc.tensor.matmul_mx(
-            out=acc[:],
-            lhsT=act_codes[:, rows].bitcast(FP8X4),
-            lhsT_scale=act_scales[:, rows],
-            rhs=wts_codes[:, cols].bitcast(FP8X4),
-            rhs_scale=wts_scales[:, cols],
-            start=(first and g == 0),
-            stop=(last and g == PASSES - 1),
-        )
-
-
-def layer_norm_act(nc, pools, neg_half, v, half_sums, gain, bias, func, result):
-    small = pools["small"]
-    scaled_sums = small.tile([P, HALVES], F32, name="scaled_sums")
-    neg_mean = small.tile([P, 1], F32, name="neg_mean")
-    nc.scalar.activation(
-        out=scaled_sums[:], in_=half_sums[:], func=ACT.Identity, scale=-1.0 / WIDTH, accum_out=neg_mean[:]
-    )
-    squares = pools["squares"].tile([P, WIDTH], BF16, name="squares")
-    sum_sq = small.tile([P, 1], F32, name="sum_sq")
-    nc.scalar.activation(out=squares[:], in_=v[:], func=ACT.Square, bias=neg_mean[:], accum_out=sum_sq[:])
-    var_eps = small.tile([P, 1], F32, name="var_eps")
-    nc.gpsimd.tensor_scalar(
-        out=var_eps[:], in0=sum_sq[:], scalar1=1.0 / WIDTH, scalar2=EPS_LN, op0=ALU.mult, op1=ALU.add
-    )
-    rstd = small.tile([P, 1], F32, name="rstd")
-    nc.gpsimd.tensor_tensor(out=rstd[:], in0=var_eps[:], in1=neg_half[:], op=ALU.pow)
-    z = pools["z"].tile([P, WIDTH], F32, name="z")
-    nc.vector.scalar_tensor_tensor(out=z[:], in0=v[:], scalar=neg_mean[:], in1=gain[:], op0=ALU.add, op1=ALU.mult)
-    nc.vector.scalar_tensor_tensor(out=z[:], in0=z[:], scalar=rstd[:], in1=bias[:], op0=ALU.mult, op1=ALU.add)
-    nc.scalar.activation(out=result[:], in_=z[:], func=func)
 
 
 def tile_rssmcell_pa_kernel(
@@ -97,19 +32,36 @@ def tile_rssmcell_pa_kernel(
 ):
     nc = tc.nc
     with ExitStack() as ctx:
-        pools = {
-            "const": ctx.enter_context(tc.tile_pool(name="const", bufs=1)),
-            "raw": ctx.enter_context(tc.tile_pool(name="raw", bufs=16)),
-            "grouped": ctx.enter_context(tc.tile_pool(name="grouped", bufs=3)),
-            "wts": ctx.enter_context(tc.tile_pool(name="wts", bufs=6)),
-            "gate": ctx.enter_context(tc.tile_pool(name="gate", bufs=ROW_TILES)),
-            "z": ctx.enter_context(tc.tile_pool(name="z", bufs=3)),
-            "squares": ctx.enter_context(tc.tile_pool(name="squares", bufs=2)),
-            "small": ctx.enter_context(tc.tile_pool(name="small", bufs=8)),
-            "turned": ctx.enter_context(tc.psum_pool(name="turned", bufs=4)),
-            "acc": ctx.enter_context(tc.psum_pool(name="acc", bufs=4)),
-        }
-        const = pools["const"]
+        const = ctx.enter_context(tc.tile_pool(name="const", bufs=1))
+        raw_pool = ctx.enter_context(tc.tile_pool(name="raw", bufs=(LOAD_AHEAD + 1) * BLOCKS))
+        grouped_pool = ctx.enter_context(tc.tile_pool(name="grouped", bufs=3))
+        gate_pool = ctx.enter_context(tc.tile_pool(name="gate", bufs=ROW_TILES))
+        z_pool = ctx.enter_context(tc.tile_pool(name="z", bufs=3))
+        squares_pool = ctx.enter_context(tc.tile_pool(name="squares", bufs=2))
+        small = ctx.enter_context(tc.tile_pool(name="small", bufs=8))
+        turned_pool = ctx.enter_context(tc.psum_pool(name="turned", bufs=4))
+        acc_pool = ctx.enter_context(tc.psum_pool(name="acc", bufs=4))
+        ctx.enter_context(tc.manual_schedule())
+
+        def weight_rows(w, gate_index, h):
+            first_row = gate_index * WIDTH + h * CHUNK
+            return w[first_row : first_row + CHUNK, :]
+
+        X, D = 0, 1
+        sources = [x_pre, deter]
+        partner = [None, None]
+        chunk_of = {}
+        for gate, gate_index, order in (("r", 0, ("ih", "hh")), ("n", 2, ("hh", "ih")), ("u", 1, ("ih", "hh"))):
+            for h in range(HALVES):
+                for which in order:
+                    chunk_of[(gate, which, h)] = len(sources)
+                    sources.append(weight_rows(w_ih if which == "ih" else w_hh, gate_index, h))
+                    partner.append(X if which == "ih" else D)
+        n_chunks = len(sources)
+        codes = [const.tile([P, PASSES * CHUNK], U32, align_bytes=64, name="codes%d" % c) for c in range(n_chunks)]
+        scales = [const.tile([P, PASSES * CHUNK], U8, align_bytes=64, name="scales%d" % c) for c in range(n_chunks)]
+        raw = {}
+        grouped = {}
 
         ident = const.tile([P, P], F32, name="ident")
         make_identity(nc, ident[:])
@@ -117,113 +69,238 @@ def tile_rssmcell_pa_kernel(
         make_identity(nc, ident_bf[:])
         neg_half = const.tile([P, 1], F32, name="neg_half")
         nc.gpsimd.memset(neg_half[:], -0.5)
-
         mask_sb = const.tile([P, ROW_TILES], BF16, name="mask_sb")
         with nc.allow_non_contiguous_dma(reason="512 mask values, one to a partition for each row tile"):
             nc.scalar.dma_start(out=mask_sb[:], in_=mask.rearrange("(m p) o -> p (m o)", p=P))
-        ln_vectors = [ln_r_g, ln_r_b, ln_u_g, ln_u_b, ln_n_g, ln_n_b]
         ln_rows = const.tile([P, WIDTH], BF16, name="ln_rows")
         nc.vector.memset(ln_rows[:], 0.0)
-        for r, vector in enumerate(ln_vectors):
-            nc.scalar.dma_start(out=ln_rows[r : r + 1, :], in_=vector.unsqueeze(0))
-
-        x_codes = const.tile([P, PASSES * CHUNK], U32, align_bytes=64, name="x_codes")
-        x_scales = const.tile([P, PASSES * CHUNK], U8, align_bytes=64, name="x_scales")
-        quantise_chunk(nc, pools, ident, load_blocks(nc, pools, x_pre), x_codes, x_scales, True)
+        nc.scalar.dma_start(out=ln_rows[0:1, :], in_=ln_r_g.unsqueeze(0))
+        nc.scalar.dma_start(out=ln_rows[1:2, :], in_=ln_r_b.unsqueeze(0))
         d_sb = const.tile([P, ROW_TILES, K], BF16, name="d_sb")
-        for m, raw in enumerate(load_blocks(nc, pools, deter)):
-            nc.vector.tensor_scalar_mul(out=d_sb[:, m, :], in0=raw, scalar1=mask_sb[:, m : m + 1])
-        d_codes = const.tile([P, PASSES * CHUNK], U32, align_bytes=64, name="d_codes")
-        d_scales = const.tile([P, PASSES * CHUNK], U8, align_bytes=64, name="d_scales")
-        quantise_chunk(nc, pools, ident, [d_sb[:, m, :] for m in range(ROW_TILES)], d_codes, d_scales, True)
-        acts = {"ih": (x_codes, x_scales), "hh": (d_codes, d_scales)}
-        weights = {"ih": w_ih, "hh": w_hh}
+        gain = {}
+        bias = {}
 
-        def weight_chunk(which, gate, h, vector_helps):
-            first_row = gate * WIDTH + h * CHUNK
-            codes = pools["wts"].tile([P, PASSES * CHUNK], U32, align_bytes=64, name="w_codes")
-            scales = pools["wts"].tile([P, PASSES * CHUNK], U8, align_bytes=64, name="w_scales")
-            blocks = load_blocks(nc, pools, weights[which][first_row : first_row + CHUNK, :])
-            quantise_chunk(nc, pools, ident, blocks, codes, scales, vector_helps)
-            return codes, scales
+        def load(c):
+            if c >= n_chunks:
+                return
+            raw[c] = []
+            for t in range(BLOCKS):
+                block = raw_pool.tile([P, K], BF16, name="raw")
+                nc.sync.dma_start(out=block[:], in_=sources[c][t * P : (t + 1) * P, :])
+                raw[c].append(block[:])
+            if c == n_chunks - 1:
+                for gate, g_vec, b_vec in (("n", ln_n_g, ln_n_b), ("u", ln_u_g, ln_u_b)):
+                    gain[gate] = const.tile([P, WIDTH], BF16, name="gain_" + gate)
+                    nc.sync.dma_start(out=gain[gate][:], in_=g_vec.partition_broadcast(P))
+                    bias[gate] = const.tile([P, WIDTH], BF16, name="bias_" + gate)
+                    nc.sync.dma_start(out=bias[gate][:], in_=b_vec.partition_broadcast(P))
 
-        def spread(r):
-            bank = pools["turned"].tile([P, WIDTH], BF16, name="bank")
+        def turn(c):
+            if c == D:
+                for m in range(ROW_TILES):
+                    nc.vector.tensor_scalar_mul(out=d_sb[:, m, :], in0=raw[D][m], scalar1=mask_sb[:, m : m + 1])
+                raw[D] = [d_sb[:, m, :] for m in range(ROW_TILES)]
+            grouped[c] = grouped_pool.tile([P, 4 * PASSES * CHUNK], BF16, align_bytes=64, name="grouped")
+            grouped_words = grouped[c][:].bitcast(F32).rearrange("p (g c u) -> p g c u", g=PASSES, u=2)
+            for t in range(BLOCKS):
+                words = raw[c][t].bitcast(F32)
+                bank = turned_pool.tile([P, CHUNK], F32, name="bank")
+                for a in range(2 * PASSES):
+                    nc.tensor.transpose(
+                        out=bank[:, a * P : (a + 1) * P], in_=words[:, a * P : (a + 1) * P], identity=ident[:]
+                    )
+                turned = bank[:].rearrange("p (g u c) -> p g c u", g=PASSES, u=2)
+                if c < VECTOR_HELPS_BEFORE and t % 2 == 1:
+                    nc.vector.tensor_copy(out=grouped_words[:, :, t * P : (t + 1) * P, :], in_=turned)
+                else:
+                    nc.scalar.copy(out=grouped_words[:, :, t * P : (t + 1) * P, :], in_=turned)
+
+        def quantise(c):
+            nc.vector.quantize_mx(out=codes[c][:].bitcast(FP8X4), scales=scales[c][:], in_=grouped[c][:])
+
+        def passes(bank, c, m, first, last):
+            a = partner[c]
+            for g in range(PASSES):
+                rows = slice(g * CHUNK + m * P, g * CHUNK + (m + 1) * P)
+                cols = slice(g * CHUNK, (g + 1) * CHUNK)
+                nc.tensor.matmul_mx(
+                    out=bank[:],
+                    lhsT=codes[a][:, rows].bitcast(FP8X4),
+                    lhsT_scale=scales[a][:, rows],
+                    rhs=codes[c][:, cols].bitcast(FP8X4),
+                    rhs_scale=scales[c][:, cols],
+                    start=(first and g == 0),
+                    stop=(last and g == PASSES - 1),
+                )
+
+        def spread(row, name):
+            bank = turned_pool.tile([P, WIDTH], BF16, name="bank")
             for h in range(HALVES):
                 cols = slice(h * CHUNK, (h + 1) * CHUNK)
                 nc.tensor.matmul(
                     out=bank[:, cols],
-                    lhsT=ident_bf[:, r : r + 1].to_broadcast([P, P]),
+                    lhsT=ident_bf[:, row : row + 1].to_broadcast([P, P]),
                     rhs=ln_rows[:, cols],
                     start=True,
                     stop=True,
                 )
-            everywhere = const.tile([P, WIDTH], BF16, name="ln_spread_%d" % r)
+            everywhere = const.tile([P, WIDTH], BF16, name=name)
             nc.vector.tensor_copy(out=everywhere[:], in_=bank[:])
             return everywhere
 
-        def summed_gate(wts, name):
-            sums = [pools["gate"].tile([P, WIDTH], F32, name=name) for m in range(ROW_TILES)]
-            half_sums = [pools["small"].tile([P, HALVES], F32, name="half_sums") for m in range(ROW_TILES)]
-            for h in range(HALVES):
-                banks = [pools["acc"].tile([P, CHUNK], F32, name="acc") for m in range(ROW_TILES)]
-                for which in ("ih", "hh"):
-                    for m in range(ROW_TILES):
-                        mx_passes(nc, banks[m], acts[which], wts[(which, h)], m, which == "ih", which == "hh")
+        jobs = [(gate, m) for gate in ("r", "n", "u") for m in range(ROW_TILES)]
+        value = {}
+        half_sums = {}
+        neg_mean = {}
+        rstd = {}
+        z = {}
+        for job in jobs:
+            value[job] = gate_pool.tile([P, WIDTH], F32, name=job[0] + "_gate")
+            half_sums[job] = small.tile([P, HALVES], F32, name="half_sums", bufs=len(jobs))
+
+        def evacuate(job, h, bank):
+            nc.scalar.activation(
+                out=value[job][:, h * CHUNK : (h + 1) * CHUNK],
+                in_=bank[:],
+                func=ACT.Identity,
+                accum_out=half_sums[job][:, h : h + 1],
+            )
+
+        open_banks = {}
+
+        def reset_chunk(c, h, first, last):
+            for m in range(ROW_TILES):
+                if first:
+                    open_banks[m] = acc_pool.tile([P, CHUNK], F32, name="acc")
+                passes(open_banks[m], c, m, first, last)
+            if last:
                 for m in range(ROW_TILES):
-                    nc.scalar.activation(
-                        out=sums[m][:, h * CHUNK : (h + 1) * CHUNK],
-                        in_=banks[m][:],
-                        func=ACT.Identity,
-                        accum_out=half_sums[m][:, h : h + 1],
+                    evacuate(("r", m), h, open_banks[m])
+
+        def gate_input(job):
+            gate, m = job
+            if gate == "r":
+                passes(open_banks[m], chunk_of[("r", "hh", 1)], m, False, True)
+                evacuate(job, 1, open_banks[m])
+            if gate == "u":
+                for h in range(HALVES):
+                    bank = acc_pool.tile([P, CHUNK], F32, name="acc")
+                    passes(bank, chunk_of[("u", "ih", h)], m, True, False)
+                    passes(bank, chunk_of[("u", "hh", h)], m, False, True)
+                    evacuate(job, h, bank)
+            if gate == "n":
+                banks = {}
+                for h in range(HALVES):
+                    for which in ("hh", "ih"):
+                        banks[(which, h)] = acc_pool.tile([P, CHUNK], F32, name="acc")
+                        passes(banks[(which, h)], chunk_of[("n", which, h)], m, True, True)
+                for h in range(HALVES):
+                    cols = slice(h * CHUNK, (h + 1) * CHUNK)
+                    nc.vector.tensor_tensor(
+                        out=value[job][:, cols], in0=value[("r", m)][:, cols], in1=banks[("hh", h)][:], op=ALU.mult
                     )
-            return sums, half_sums
+                for h in range(HALVES):
+                    cols = slice(h * CHUNK, (h + 1) * CHUNK)
+                    nc.vector.scalar_tensor_tensor(
+                        out=value[job][:, cols],
+                        in0=value[job][:, cols],
+                        scalar=1.0,
+                        in1=banks[("ih", h)][:],
+                        op0=ALU.mult,
+                        op1=ALU.add,
+                        accum_out=half_sums[job][:, h : h + 1],
+                    )
 
-        r_gain, r_bias, u_gain, u_bias, n_gain, n_bias = [spread(r) for r in range(len(ln_vectors))]
+        def statistics(job):
+            scaled_sums = small.tile([P, HALVES], F32, name="scaled_sums")
+            neg_mean[job] = small.tile([P, 1], F32, name="neg_mean")
+            nc.scalar.activation(
+                out=scaled_sums[:],
+                in_=half_sums[job][:],
+                func=ACT.Identity,
+                scale=-1.0 / WIDTH,
+                accum_out=neg_mean[job][:],
+            )
+            squares = squares_pool.tile([P, WIDTH], BF16, name="squares")
+            sum_sq = small.tile([P, 1], F32, name="sum_sq")
+            nc.scalar.activation(
+                out=squares[:], in_=value[job][:], func=ACT.Square, bias=neg_mean[job][:], accum_out=sum_sq[:]
+            )
+            var_eps = small.tile([P, 1], F32, name="var_eps")
+            nc.gpsimd.tensor_scalar(
+                out=var_eps[:], in0=sum_sq[:], scalar1=1.0 / WIDTH, scalar2=EPS_LN, op0=ALU.mult, op1=ALU.add
+            )
+            rstd[job] = small.tile([P, 1], F32, name="rstd")
+            nc.gpsimd.tensor_tensor(out=rstd[job][:], in0=var_eps[:], in1=neg_half[:], op=ALU.pow)
 
-        summed_order = [("ih", 0), ("hh", 0), ("ih", 1), ("hh", 1)]
-        candidate_order = [("hh", 0), ("ih", 0), ("hh", 1), ("ih", 1)]
+        def centre(job):
+            z[job] = z_pool.tile([P, WIDTH], F32, name="z")
+            nc.vector.scalar_tensor_tensor(
+                out=z[job][:],
+                in0=value[job][:],
+                scalar=neg_mean[job][:],
+                in1=gain[job[0]][:],
+                op0=ALU.add,
+                op1=ALU.mult,
+            )
 
-        wts = {}
-        for which, h in summed_order:
-            wts[(which, h)] = weight_chunk(which, GATE_R, h, True)
-        reset, half_sums = summed_gate(wts, "r_gate")
-        wts = {}
-        for m in range(ROW_TILES):
-            which, h = candidate_order[m]
-            wts[(which, h)] = weight_chunk(which, GATE_N, h, False)
-            layer_norm_act(nc, pools, neg_half, reset[m], half_sums[m], r_gain, r_bias, ACT.Sigmoid, reset[m])
+        def affine(job):
+            nc.vector.scalar_tensor_tensor(
+                out=z[job][:], in0=z[job][:], scalar=rstd[job][:], in1=bias[job[0]][:], op0=ALU.mult, op1=ALU.add
+            )
 
-        blend = [pools["gate"].tile([P, WIDTH], F32, name="n_gate") for m in range(ROW_TILES)]
-        pre_sums = [pools["small"].tile([P, HALVES], F32, name="pre_sums") for m in range(ROW_TILES)]
-        for h in range(HALVES):
-            cols = slice(h * CHUNK, (h + 1) * CHUNK)
-            for m in range(ROW_TILES):
-                acc = pools["acc"].tile([P, CHUNK], F32, name="acc")
-                mx_passes(nc, acc, acts["hh"], wts[("hh", h)], m, True, True)
-                nc.vector.tensor_tensor(out=blend[m][:, cols], in0=reset[m][:, cols], in1=acc[:], op=ALU.mult)
-            for m in range(ROW_TILES):
-                acc = pools["acc"].tile([P, CHUNK], F32, name="acc")
-                mx_passes(nc, acc, acts["ih"], wts[("ih", h)], m, True, True)
-                nc.vector.scalar_tensor_tensor(
-                    out=blend[m][:, cols],
-                    in0=blend[m][:, cols],
-                    scalar=1.0,
-                    in1=acc[:],
-                    op0=ALU.mult,
-                    op1=ALU.add,
-                    accum_out=pre_sums[m][:, h : h + 1],
-                )
-        wts = {}
-        for m in range(ROW_TILES):
-            which, h = summed_order[m]
-            wts[(which, h)] = weight_chunk(which, GATE_U, h, False)
-            layer_norm_act(nc, pools, neg_half, blend[m], pre_sums[m], n_gain, n_bias, ACT.Tanh, blend[m])
-            nc.vector.tensor_tensor(out=blend[m][:], in0=blend[m][:], in1=d_sb[:, m, :], op=ALU.subtract)
+        def activate(job):
+            func = ACT.Tanh if job[0] == "n" else ACT.Sigmoid
+            nc.scalar.activation(out=value[job][:], in_=z[job][:], func=func)
 
-        update, half_sums = summed_gate(wts, "u_gate")
-        for m in range(ROW_TILES):
-            layer_norm_act(nc, pools, neg_half, update[m], half_sums[m], u_gain, u_bias, ACT.Sigmoid, update[m])
-            nc.vector.tensor_tensor(out=blend[m][:], in0=blend[m][:], in1=update[m][:], op=ALU.mult)
-            nc.vector.tensor_tensor(out=blend[m][:], in0=blend[m][:], in1=d_sb[:, m, :], op=ALU.add)
-            nc.sync.dma_start(out=out[m * P : (m + 1) * P, :], in_=blend[m][:])
+        def blend(job):
+            gate, m = job
+            mix = value[("n", m)]
+            if gate == "n":
+                nc.vector.tensor_tensor(out=mix[:], in0=mix[:], in1=d_sb[:, m, :], op=ALU.subtract)
+            if gate == "u":
+                nc.vector.tensor_tensor(out=mix[:], in0=mix[:], in1=value[job][:], op=ALU.mult)
+                nc.vector.tensor_tensor(out=mix[:], in0=mix[:], in1=d_sb[:, m, :], op=ALU.add)
+                nc.sync.dma_start(out=out[m * P : (m + 1) * P, :], in_=mix[:])
+
+        head_chunks = chunk_of[("r", "hh", 1)] + 1
+        for c in range(LOAD_AHEAD):
+            load(c)
+        for c in range(head_chunks):
+            load(c + LOAD_AHEAD)
+            if c == chunk_of[("r", "ih", 1)]:
+                reset_chunk(chunk_of[("r", "ih", 0)], 0, True, False)
+            if c == chunk_of[("r", "hh", 1)]:
+                reset_chunk(chunk_of[("r", "hh", 0)], 0, False, True)
+            turn(c)
+            quantise(c)
+            if c == D:
+                gain["r"] = spread(0, "gain_r")
+                bias["r"] = spread(1, "bias_r")
+        reset_chunk(chunk_of[("r", "ih", 1)], 1, True, False)
+
+        def job_at(index):
+            return jobs[index] if 0 <= index < len(jobs) else None
+
+        for step in range(-1, len(jobs) + 3):
+            c = head_chunks + step + 1
+            if job_at(step):
+                statistics(job_at(step))
+            coming = job_at(step + 1)
+            if coming and coming[0] == "r":
+                gate_input(coming)
+            if c < n_chunks:
+                load(c + LOAD_AHEAD)
+                turn(c)
+            if job_at(step - 1):
+                centre(job_at(step - 1))
+            if head_chunks <= c - 1 < n_chunks:
+                quantise(c - 1)
+            if job_at(step - 1):
+                affine(job_at(step - 1))
+            if coming and coming[0] != "r":
+                gate_input(coming)
+            if job_at(step - 2):
+                activate(job_at(step - 2))
+            if job_at(step - 3):
+                blend(job_at(step - 3))

@@ -40,7 +40,8 @@ def tile_rssmcell_pa_kernel(
         squares_pool = ctx.enter_context(tc.tile_pool(name="squares", bufs=2))
         small = ctx.enter_context(tc.tile_pool(name="small", bufs=8))
         turned_pool = ctx.enter_context(tc.psum_pool(name="turned", bufs=4))
-        acc_pool = ctx.enter_context(tc.psum_pool(name="acc", bufs=4))
+        acc_pool = ctx.enter_context(tc.psum_pool(name="acc", bufs=3))
+        gain_pool = ctx.enter_context(tc.psum_pool(name="gain", bufs=1))
         ctx.enter_context(tc.manual_schedule())
 
         def weight_rows(w, gate_index, h):
@@ -74,8 +75,10 @@ def tile_rssmcell_pa_kernel(
             nc.scalar.dma_start(out=mask_sb[:], in_=mask.rearrange("(m p) o -> p (m o)", p=P))
         ln_rows = const.tile([P, WIDTH], BF16, name="ln_rows")
         nc.vector.memset(ln_rows[:], 0.0)
-        nc.scalar.dma_start(out=ln_rows[0:1, :], in_=ln_r_g.unsqueeze(0))
-        nc.scalar.dma_start(out=ln_rows[1:2, :], in_=ln_r_b.unsqueeze(0))
+        ln_row_of = {"gain_r": 0, "gain_n": 1, "gain_u": 2, "bias_r": 3}
+        for name, vector in (("gain_r", ln_r_g), ("gain_n", ln_n_g), ("gain_u", ln_u_g), ("bias_r", ln_r_b)):
+            row = ln_row_of[name]
+            nc.scalar.dma_start(out=ln_rows[row : row + 1, :], in_=vector.unsqueeze(0))
         d_sb = const.tile([P, ROW_TILES, K], BF16, name="d_sb")
         gain = {}
         bias = {}
@@ -89,9 +92,7 @@ def tile_rssmcell_pa_kernel(
                 nc.sync.dma_start(out=block[:], in_=sources[c][t * P : (t + 1) * P, :])
                 raw[c].append(block[:])
             if c == n_chunks - 1:
-                for gate, g_vec, b_vec in (("n", ln_n_g, ln_n_b), ("u", ln_u_g, ln_u_b)):
-                    gain[gate] = const.tile([P, WIDTH], BF16, name="gain_" + gate)
-                    nc.sync.dma_start(out=gain[gate][:], in_=g_vec.partition_broadcast(P))
+                for gate, b_vec in (("n", ln_n_b), ("u", ln_u_b)):
                     bias[gate] = const.tile([P, WIDTH], BF16, name="bias_" + gate)
                     nc.sync.dma_start(out=bias[gate][:], in_=b_vec.partition_broadcast(P))
 
@@ -133,8 +134,9 @@ def tile_rssmcell_pa_kernel(
                     stop=(last and g == PASSES - 1),
                 )
 
-        def spread(row, name):
-            bank = turned_pool.tile([P, WIDTH], BF16, name="bank")
+        def spread(name, pool):
+            row = ln_row_of[name]
+            bank = pool.tile([P, WIDTH], BF16, name="bank")
             for h in range(HALVES):
                 cols = slice(h * CHUNK, (h + 1) * CHUNK)
                 nc.tensor.matmul(
@@ -144,9 +146,7 @@ def tile_rssmcell_pa_kernel(
                     start=True,
                     stop=True,
                 )
-            everywhere = const.tile([P, WIDTH], BF16, name=name)
-            nc.vector.tensor_copy(out=everywhere[:], in_=bank[:])
-            return everywhere
+            return bank
 
         jobs = [(gate, m) for gate in ("r", "n", "u") for m in range(ROW_TILES)]
         value = {}
@@ -166,27 +166,13 @@ def tile_rssmcell_pa_kernel(
                 accum_out=half_sums[job][:, h : h + 1],
             )
 
-        open_banks = {}
-
-        def reset_chunk(c, h, first, last):
-            for m in range(ROW_TILES):
-                if first:
-                    open_banks[m] = acc_pool.tile([P, CHUNK], F32, name="acc")
-                passes(open_banks[m], c, m, first, last)
-            if last:
-                for m in range(ROW_TILES):
-                    evacuate(("r", m), h, open_banks[m])
-
         def gate_input(job):
             gate, m = job
-            if gate == "r":
-                passes(open_banks[m], chunk_of[("r", "hh", 1)], m, False, True)
-                evacuate(job, 1, open_banks[m])
-            if gate == "u":
+            if gate != "n":
                 for h in range(HALVES):
                     bank = acc_pool.tile([P, CHUNK], F32, name="acc")
-                    passes(bank, chunk_of[("u", "ih", h)], m, True, False)
-                    passes(bank, chunk_of[("u", "hh", h)], m, False, True)
+                    passes(bank, chunk_of[(gate, "ih", h)], m, True, False)
+                    passes(bank, chunk_of[(gate, "hh", h)], m, False, True)
                     evacuate(job, h, bank)
             if gate == "n":
                 banks = {}
@@ -194,7 +180,6 @@ def tile_rssmcell_pa_kernel(
                     for which in ("hh", "ih"):
                         banks[(which, h)] = acc_pool.tile([P, CHUNK], F32, name="acc")
                         passes(banks[(which, h)], chunk_of[("n", which, h)], m, True, True)
-                for h in range(HALVES):
                     cols = slice(h * CHUNK, (h + 1) * CHUNK)
                     nc.vector.tensor_tensor(
                         out=value[job][:, cols], in0=value[("r", m)][:, cols], in1=banks[("hh", h)][:], op=ALU.mult
@@ -243,6 +228,9 @@ def tile_rssmcell_pa_kernel(
                 op0=ALU.add,
                 op1=ALU.mult,
             )
+            following = {"r": "n", "n": "u"}
+            if job[1] == ROW_TILES - 1 and job[0] in following:
+                gain[following[job[0]]] = spread("gain_" + following[job[0]], gain_pool)
 
         def affine(job):
             nc.vector.scalar_tensor_tensor(
@@ -268,16 +256,12 @@ def tile_rssmcell_pa_kernel(
             load(c)
         for c in range(head_chunks):
             load(c + LOAD_AHEAD)
-            if c == chunk_of[("r", "ih", 1)]:
-                reset_chunk(chunk_of[("r", "ih", 0)], 0, True, False)
-            if c == chunk_of[("r", "hh", 1)]:
-                reset_chunk(chunk_of[("r", "hh", 0)], 0, False, True)
             turn(c)
             quantise(c)
             if c == D:
-                gain["r"] = spread(0, "gain_r")
-                bias["r"] = spread(1, "bias_r")
-        reset_chunk(chunk_of[("r", "ih", 1)], 1, True, False)
+                gain["r"] = spread("gain_r", gain_pool)
+                bias["r"] = const.tile([P, WIDTH], BF16, name="bias_r")
+                nc.vector.tensor_copy(out=bias["r"][:], in_=spread("bias_r", turned_pool)[:])
 
         def job_at(index):
             return jobs[index] if 0 <= index < len(jobs) else None
@@ -286,9 +270,6 @@ def tile_rssmcell_pa_kernel(
             c = head_chunks + step + 1
             if job_at(step):
                 statistics(job_at(step))
-            coming = job_at(step + 1)
-            if coming and coming[0] == "r":
-                gate_input(coming)
             if c < n_chunks:
                 load(c + LOAD_AHEAD)
                 turn(c)
@@ -298,8 +279,8 @@ def tile_rssmcell_pa_kernel(
                 quantise(c - 1)
             if job_at(step - 1):
                 affine(job_at(step - 1))
-            if coming and coming[0] != "r":
-                gate_input(coming)
+            if job_at(step + 1):
+                gate_input(job_at(step + 1))
             if job_at(step - 2):
                 activate(job_at(step - 2))
             if job_at(step - 3):

@@ -22,7 +22,7 @@ ROW_TILES = BATCH // P
 HALVES = WIDTH // CHUNK
 EPS_LN = 1e-3
 LOAD_AHEAD = 3
-VECTOR_HELPS_BEFORE = 8
+VECTOR_HELPS_BEFORE = 10
 
 FLOPS = 2 * 2 * BATCH * K * 3 * WIDTH
 
@@ -40,21 +40,23 @@ def tile_rssmcell_pa_kernel(
         squares_pool = ctx.enter_context(tc.tile_pool(name="squares", bufs=2))
         small = ctx.enter_context(tc.tile_pool(name="small", bufs=8))
         turned_pool = ctx.enter_context(tc.psum_pool(name="turned", bufs=4))
-        acc_pool = ctx.enter_context(tc.psum_pool(name="acc", bufs=3))
-        gain_pool = ctx.enter_context(tc.psum_pool(name="gain", bufs=1))
+        acc_pool = ctx.enter_context(tc.psum_pool(name="acc", bufs=4))
         ctx.enter_context(tc.manual_schedule())
 
         def weight_rows(w, gate_index, h):
             first_row = gate_index * WIDTH + h * CHUNK
             return w[first_row : first_row + CHUNK, :]
 
-        X, D = 0, 1
-        sources = [x_pre, deter]
-        partner = [None, None]
+        X, D = 0, 2
+        sources = [x_pre]
+        partner = [None]
         chunk_of = {}
         for gate, gate_index, order in (("r", 0, ("ih", "hh")), ("n", 2, ("hh", "ih")), ("u", 1, ("ih", "hh"))):
             for h in range(HALVES):
                 for which in order:
+                    if len(sources) == D:
+                        sources.append(deter)
+                        partner.append(None)
                     chunk_of[(gate, which, h)] = len(sources)
                     sources.append(weight_rows(w_ih if which == "ih" else w_hh, gate_index, h))
                     partner.append(X if which == "ih" else D)
@@ -75,10 +77,8 @@ def tile_rssmcell_pa_kernel(
             nc.scalar.dma_start(out=mask_sb[:], in_=mask.rearrange("(m p) o -> p (m o)", p=P))
         ln_rows = const.tile([P, WIDTH], BF16, name="ln_rows")
         nc.vector.memset(ln_rows[:], 0.0)
-        ln_row_of = {"gain_r": 0, "gain_n": 1, "gain_u": 2, "bias_r": 3}
-        for name, vector in (("gain_r", ln_r_g), ("gain_n", ln_n_g), ("gain_u", ln_u_g), ("bias_r", ln_r_b)):
-            row = ln_row_of[name]
-            nc.scalar.dma_start(out=ln_rows[row : row + 1, :], in_=vector.unsqueeze(0))
+        nc.scalar.dma_start(out=ln_rows[0:1, :], in_=ln_r_g.unsqueeze(0))
+        nc.scalar.dma_start(out=ln_rows[1:2, :], in_=ln_r_b.unsqueeze(0))
         d_sb = const.tile([P, ROW_TILES, K], BF16, name="d_sb")
         gain = {}
         bias = {}
@@ -92,15 +92,13 @@ def tile_rssmcell_pa_kernel(
                 nc.sync.dma_start(out=block[:], in_=sources[c][t * P : (t + 1) * P, :])
                 raw[c].append(block[:])
             if c == n_chunks - 1:
-                for gate, b_vec in (("n", ln_n_b), ("u", ln_u_b)):
+                for gate, g_vec, b_vec in (("n", ln_n_g, ln_n_b), ("u", ln_u_g, ln_u_b)):
+                    gain[gate] = const.tile([P, WIDTH], BF16, name="gain_" + gate)
+                    nc.sync.dma_start(out=gain[gate][:], in_=g_vec.partition_broadcast(P))
                     bias[gate] = const.tile([P, WIDTH], BF16, name="bias_" + gate)
                     nc.sync.dma_start(out=bias[gate][:], in_=b_vec.partition_broadcast(P))
 
         def turn(c):
-            if c == D:
-                for m in range(ROW_TILES):
-                    nc.vector.tensor_scalar_mul(out=d_sb[:, m, :], in0=raw[D][m], scalar1=mask_sb[:, m : m + 1])
-                raw[D] = [d_sb[:, m, :] for m in range(ROW_TILES)]
             grouped[c] = grouped_pool.tile([P, 4 * PASSES * CHUNK], BF16, align_bytes=64, name="grouped")
             grouped_words = grouped[c][:].bitcast(F32).rearrange("p (g c u) -> p g c u", g=PASSES, u=2)
             for t in range(BLOCKS):
@@ -111,10 +109,15 @@ def tile_rssmcell_pa_kernel(
                         out=bank[:, a * P : (a + 1) * P], in_=words[:, a * P : (a + 1) * P], identity=ident[:]
                     )
                 turned = bank[:].rearrange("p (g u c) -> p g c u", g=PASSES, u=2)
-                if c < VECTOR_HELPS_BEFORE and t % 2 == 1:
+                if c < VECTOR_HELPS_BEFORE and t == BLOCKS - 1:
                     nc.vector.tensor_copy(out=grouped_words[:, :, t * P : (t + 1) * P, :], in_=turned)
                 else:
                     nc.scalar.copy(out=grouped_words[:, :, t * P : (t + 1) * P, :], in_=turned)
+
+        def mask_state():
+            for m in range(ROW_TILES):
+                nc.vector.tensor_scalar_mul(out=d_sb[:, m, :], in0=raw[D][m], scalar1=mask_sb[:, m : m + 1])
+            raw[D] = [d_sb[:, m, :] for m in range(ROW_TILES)]
 
         def quantise(c):
             nc.vector.quantize_mx(out=codes[c][:].bitcast(FP8X4), scales=scales[c][:], in_=grouped[c][:])
@@ -134,9 +137,8 @@ def tile_rssmcell_pa_kernel(
                     stop=(last and g == PASSES - 1),
                 )
 
-        def spread(name, pool):
-            row = ln_row_of[name]
-            bank = pool.tile([P, WIDTH], BF16, name="bank")
+        def spread(row, name):
+            bank = turned_pool.tile([P, WIDTH], BF16, name="bank")
             for h in range(HALVES):
                 cols = slice(h * CHUNK, (h + 1) * CHUNK)
                 nc.tensor.matmul(
@@ -146,7 +148,9 @@ def tile_rssmcell_pa_kernel(
                     start=True,
                     stop=True,
                 )
-            return bank
+            everywhere = const.tile([P, WIDTH], BF16, name=name)
+            nc.vector.tensor_copy(out=everywhere[:], in_=bank[:])
+            return everywhere
 
         jobs = [(gate, m) for gate in ("r", "n", "u") for m in range(ROW_TILES)]
         value = {}
@@ -228,9 +232,6 @@ def tile_rssmcell_pa_kernel(
                 op0=ALU.add,
                 op1=ALU.mult,
             )
-            following = {"r": "n", "n": "u"}
-            if job[1] == ROW_TILES - 1 and job[0] in following:
-                gain[following[job[0]]] = spread("gain_" + following[job[0]], gain_pool)
 
         def affine(job):
             nc.vector.scalar_tensor_tensor(
@@ -247,9 +248,12 @@ def tile_rssmcell_pa_kernel(
             if gate == "n":
                 nc.vector.tensor_tensor(out=mix[:], in0=mix[:], in1=d_sb[:, m, :], op=ALU.subtract)
             if gate == "u":
-                nc.vector.tensor_tensor(out=mix[:], in0=mix[:], in1=value[job][:], op=ALU.mult)
-                nc.vector.tensor_tensor(out=mix[:], in0=mix[:], in1=d_sb[:, m, :], op=ALU.add)
-                nc.sync.dma_start(out=out[m * P : (m + 1) * P, :], in_=mix[:])
+                halves = [slice(h * CHUNK, (h + 1) * CHUNK) for h in range(HALVES)]
+                for cols in halves:
+                    nc.vector.tensor_tensor(out=mix[:, cols], in0=mix[:, cols], in1=value[job][:, cols], op=ALU.mult)
+                for cols in halves:
+                    nc.vector.tensor_tensor(out=mix[:, cols], in0=mix[:, cols], in1=d_sb[:, m, cols], op=ALU.add)
+                    nc.sync.dma_start(out=out[m * P : (m + 1) * P, cols], in_=mix[:, cols])
 
         head_chunks = chunk_of[("r", "hh", 1)] + 1
         for c in range(LOAD_AHEAD):
@@ -257,31 +261,32 @@ def tile_rssmcell_pa_kernel(
         for c in range(head_chunks):
             load(c + LOAD_AHEAD)
             turn(c)
+            if c == D - 1:
+                mask_state()
             quantise(c)
-            if c == D:
-                gain["r"] = spread("gain_r", gain_pool)
-                bias["r"] = const.tile([P, WIDTH], BF16, name="bias_r")
-                nc.vector.tensor_copy(out=bias["r"][:], in_=spread("bias_r", turned_pool)[:])
+        gain["r"] = spread(0, "gain_r")
+        bias["r"] = spread(1, "bias_r")
 
         def job_at(index):
             return jobs[index] if 0 <= index < len(jobs) else None
 
+        gate_input(jobs[0])
         for step in range(-1, len(jobs) + 3):
             c = head_chunks + step + 1
             if job_at(step):
                 statistics(job_at(step))
-            if c < n_chunks:
-                load(c + LOAD_AHEAD)
-                turn(c)
             if job_at(step - 1):
                 centre(job_at(step - 1))
             if head_chunks <= c - 1 < n_chunks:
                 quantise(c - 1)
+            if c < n_chunks:
+                load(c + LOAD_AHEAD)
+                turn(c)
             if job_at(step - 1):
                 affine(job_at(step - 1))
-            if job_at(step + 1):
-                gate_input(job_at(step + 1))
             if job_at(step - 2):
                 activate(job_at(step - 2))
+            if step >= 0 and job_at(step + 1):
+                gate_input(job_at(step + 1))
             if job_at(step - 3):
                 blend(job_at(step - 3))

@@ -279,14 +279,14 @@ def tile_rssmcell_pa_kernel(
                 centre(job_at(step - 1))
             if head_chunks <= c - 1 < n_chunks:
                 quantise(c - 1)
+            if job_at(step - 3):
+                blend(job_at(step - 3))
+            if job_at(step - 1):
+                affine(job_at(step - 1))
             if c < n_chunks:
                 load(c + LOAD_AHEAD)
                 turn(c)
-            if job_at(step - 1):
-                affine(job_at(step - 1))
             if job_at(step - 2):
                 activate(job_at(step - 2))
             if step >= 0 and job_at(step + 1):
                 gate_input(job_at(step + 1))
-            if job_at(step - 3):
-                blend(job_at(step - 3))

@@ -98,7 +98,7 @@ def tile_rssmcell_pa_kernel(
                     bias[gate] = const.tile([P, WIDTH], BF16, name="bias_" + gate)
                     nc.sync.dma_start(out=bias[gate][:], in_=b_vec.partition_broadcast(P))
 
-        def turn(c):
+        def turn(c, between=()):
             grouped[c] = grouped_pool.tile([P, 4 * PASSES * CHUNK], BF16, align_bytes=64, name="grouped")
             grouped_words = grouped[c][:].bitcast(F32).rearrange("p (g c u) -> p g c u", g=PASSES, u=2)
             for t in range(BLOCKS):
@@ -113,6 +113,8 @@ def tile_rssmcell_pa_kernel(
                     nc.vector.tensor_copy(out=grouped_words[:, :, t * P : (t + 1) * P, :], in_=turned)
                 else:
                     nc.scalar.copy(out=grouped_words[:, :, t * P : (t + 1) * P, :], in_=turned)
+                if t < len(between):
+                    between[t]()
 
         def mask_state():
             for m in range(ROW_TILES):
@@ -170,23 +172,34 @@ def tile_rssmcell_pa_kernel(
                 accum_out=half_sums[job][:, h : h + 1],
             )
 
+        banks = {}
+
+        def gate_sums(job):
+            gate, m = job
+
+            def pair(which, h, first, last):
+                def run():
+                    key = (job, which if gate == "n" else "sum", h)
+                    if first:
+                        banks[key] = acc_pool.tile([P, CHUNK], F32, name="acc")
+                    passes(banks[key], chunk_of[(gate, which, h)], m, first, last)
+
+                return run
+
+            if gate == "n":
+                return [pair(which, h, True, True) for h in range(HALVES) for which in ("hh", "ih")]
+            return [pair(which, h, which == "ih", which == "hh") for h in range(HALVES) for which in ("ih", "hh")]
+
         def gate_input(job):
             gate, m = job
             if gate != "n":
                 for h in range(HALVES):
-                    bank = acc_pool.tile([P, CHUNK], F32, name="acc")
-                    passes(bank, chunk_of[(gate, "ih", h)], m, True, False)
-                    passes(bank, chunk_of[(gate, "hh", h)], m, False, True)
-                    evacuate(job, h, bank)
+                    evacuate(job, h, banks[(job, "sum", h)])
             if gate == "n":
-                banks = {}
                 for h in range(HALVES):
-                    for which in ("hh", "ih"):
-                        banks[(which, h)] = acc_pool.tile([P, CHUNK], F32, name="acc")
-                        passes(banks[(which, h)], chunk_of[("n", which, h)], m, True, True)
                     cols = slice(h * CHUNK, (h + 1) * CHUNK)
                     nc.vector.tensor_tensor(
-                        out=value[job][:, cols], in0=value[("r", m)][:, cols], in1=banks[("hh", h)][:], op=ALU.mult
+                        out=value[job][:, cols], in0=value[("r", m)][:, cols], in1=banks[(job, "hh", h)][:], op=ALU.mult
                     )
                 for h in range(HALVES):
                     cols = slice(h * CHUNK, (h + 1) * CHUNK)
@@ -194,7 +207,7 @@ def tile_rssmcell_pa_kernel(
                         out=value[job][:, cols],
                         in0=value[job][:, cols],
                         scalar=1.0,
-                        in1=banks[("ih", h)][:],
+                        in1=banks[(job, "ih", h)][:],
                         op0=ALU.mult,
                         op1=ALU.add,
                         accum_out=half_sums[job][:, h : h + 1],
@@ -270,6 +283,8 @@ def tile_rssmcell_pa_kernel(
         def job_at(index):
             return jobs[index] if 0 <= index < len(jobs) else None
 
+        for sums in gate_sums(jobs[0]):
+            sums()
         gate_input(jobs[0])
         for step in range(-1, len(jobs) + 3):
             c = head_chunks + step + 1
@@ -283,10 +298,15 @@ def tile_rssmcell_pa_kernel(
                 blend(job_at(step - 3))
             if job_at(step - 1):
                 affine(job_at(step - 1))
+            following = job_at(step + 1) if step >= 0 else None
+            sums = gate_sums(following) if following else []
             if c < n_chunks:
                 load(c + LOAD_AHEAD)
-                turn(c)
+                turn(c, sums)
+            else:
+                for pair in sums:
+                    pair()
             if job_at(step - 2):
                 activate(job_at(step - 2))
-            if step >= 0 and job_at(step + 1):
-                gate_input(job_at(step + 1))
+            if following:
+                gate_input(following)

@@ -22,7 +22,7 @@ ROW_TILES = BATCH // P
 HALVES = WIDTH // CHUNK
 EPS_LN = 1e-3
 LOAD_AHEAD = 3
-VECTOR_HELPS_BEFORE = 10
+VECTOR_HELPS_BEFORE = 6
 
 FLOPS = 2 * 2 * BATCH * K * 3 * WIDTH
 
@@ -72,13 +72,24 @@ def tile_rssmcell_pa_kernel(
         make_identity(nc, ident_bf[:])
         neg_half = const.tile([P, 1], F32, name="neg_half")
         nc.gpsimd.memset(neg_half[:], -0.5)
+        warm = const.tile([P, 1], F32, name="warm")
+        nc.vector.memset(warm[:], 0.0)
+        ln_rows = const.tile([P, WIDTH], BF16, name="ln_rows")
+        nc.vector.memset(ln_rows[:], 0.0)
+        nc.scalar.activation(out=warm[:], in_=warm[:], func=ACT.Sigmoid)
         mask_sb = const.tile([P, ROW_TILES], BF16, name="mask_sb")
         with nc.allow_non_contiguous_dma(reason="512 mask values, one to a partition for each row tile"):
             nc.scalar.dma_start(out=mask_sb[:], in_=mask.rearrange("(m p) o -> p (m o)", p=P))
-        ln_rows = const.tile([P, WIDTH], BF16, name="ln_rows")
-        nc.vector.memset(ln_rows[:], 0.0)
-        nc.scalar.dma_start(out=ln_rows[0:1, :], in_=ln_r_g.unsqueeze(0))
-        nc.scalar.dma_start(out=ln_rows[1:2, :], in_=ln_r_b.unsqueeze(0))
+        vectors = {
+            ("r", "gain"): ln_r_g,
+            ("r", "bias"): ln_r_b,
+            ("n", "gain"): ln_n_g,
+            ("n", "bias"): ln_n_b,
+            ("u", "gain"): ln_u_g,
+            ("u", "bias"): ln_u_b,
+        }
+        for row, vec in enumerate(vectors.values()):
+            nc.scalar.dma_start(out=ln_rows[row : row + 1, :], in_=vec.unsqueeze(0))
         d_sb = const.tile([P, ROW_TILES, K], BF16, name="d_sb")
         gain = {}
         bias = {}
@@ -91,12 +102,6 @@ def tile_rssmcell_pa_kernel(
                 block = raw_pool.tile([P, K], BF16, name="raw")
                 nc.sync.dma_start(out=block[:], in_=sources[c][t * P : (t + 1) * P, :])
                 raw[c].append(block[:])
-            if c == n_chunks - 1:
-                for gate, g_vec, b_vec in (("n", ln_n_g, ln_n_b), ("u", ln_u_g, ln_u_b)):
-                    gain[gate] = const.tile([P, WIDTH], BF16, name="gain_" + gate)
-                    nc.sync.dma_start(out=gain[gate][:], in_=g_vec.partition_broadcast(P))
-                    bias[gate] = const.tile([P, WIDTH], BF16, name="bias_" + gate)
-                    nc.sync.dma_start(out=bias[gate][:], in_=b_vec.partition_broadcast(P))
 
         def turn(c, between=()):
             grouped[c] = grouped_pool.tile([P, 4 * PASSES * CHUNK], BF16, align_bytes=64, name="grouped")
@@ -139,7 +144,8 @@ def tile_rssmcell_pa_kernel(
                     stop=(last and g == PASSES - 1),
                 )
 
-        def spread(row, name):
+        def spread(gate, kind):
+            row = list(vectors).index((gate, kind))
             bank = turned_pool.tile([P, WIDTH], BF16, name="bank")
             for h in range(HALVES):
                 cols = slice(h * CHUNK, (h + 1) * CHUNK)
@@ -150,8 +156,11 @@ def tile_rssmcell_pa_kernel(
                     start=True,
                     stop=True,
                 )
-            everywhere = const.tile([P, WIDTH], BF16, name=name)
-            nc.vector.tensor_copy(out=everywhere[:], in_=bank[:])
+            everywhere = const.tile([P, WIDTH], BF16, name=kind + "_" + gate)
+            if kind == "gain":
+                nc.scalar.copy(out=everywhere[:], in_=bank[:])
+            else:
+                nc.vector.tensor_copy(out=everywhere[:], in_=bank[:])
             return everywhere
 
         jobs = [(gate, m) for gate in ("r", "n", "u") for m in range(ROW_TILES)]
@@ -277,8 +286,10 @@ def tile_rssmcell_pa_kernel(
             if c == D - 1:
                 mask_state()
             quantise(c)
-        gain["r"] = spread(0, "gain_r")
-        bias["r"] = spread(1, "bias_r")
+            gate = {1: "r", 3: "n", 5: "u"}.get(c)
+            if gate:
+                gain[gate] = spread(gate, "gain")
+                bias[gate] = spread(gate, "bias")
 
         def job_at(index):
             return jobs[index] if 0 <= index < len(jobs) else None

@@ -70,6 +70,10 @@ def tile_rssmcell_pa_kernel(
         make_identity(nc, ident[:])
         ident_bf = const.tile([P, P], BF16, name="ident_bf")
         make_identity(nc, ident_bf[:])
+        neg_ident_bf = const.tile([P, P], BF16, name="neg_ident_bf")
+        nc.gpsimd.tensor_scalar(
+            out=neg_ident_bf[:], in0=ident_bf[:], scalar1=-1.0, scalar2=0.0, op0=ALU.mult, op1=ALU.add
+        )
         neg_half = const.tile([P, 1], F32, name="neg_half")
         nc.gpsimd.memset(neg_half[:], -0.5)
         warm = const.tile([P, 1], F32, name="warm")
@@ -264,15 +268,25 @@ def tile_rssmcell_pa_kernel(
             func = ACT.Tanh if job[0] == "n" else ACT.Sigmoid
             nc.scalar.activation(out=value[job][:], in_=z[job][:], func=func)
 
+        differences = {}
+
+        def difference(m):
+            for h in range(HALVES):
+                cols = slice(h * CHUNK, (h + 1) * CHUNK)
+                bank = turned_pool.tile([P, CHUNK], F32, name="bank")
+                nc.tensor.matmul(out=bank[:], lhsT=ident[:], rhs=value[("n", m)][:, cols], start=True, stop=False)
+                nc.tensor.matmul(out=bank[:], lhsT=neg_ident_bf[:], rhs=d_sb[:, m, cols], start=False, stop=True)
+                differences[(m, h)] = bank
+
         def blend(job):
             gate, m = job
             mix = value[("n", m)]
-            if gate == "n":
-                nc.vector.tensor_tensor(out=mix[:], in0=mix[:], in1=d_sb[:, m, :], op=ALU.subtract)
             if gate == "u":
                 halves = [slice(h * CHUNK, (h + 1) * CHUNK) for h in range(HALVES)]
-                for cols in halves:
-                    nc.vector.tensor_tensor(out=mix[:, cols], in0=mix[:, cols], in1=value[job][:, cols], op=ALU.mult)
+                for h, cols in enumerate(halves):
+                    nc.vector.tensor_tensor(
+                        out=mix[:, cols], in0=value[job][:, cols], in1=differences[(m, h)][:], op=ALU.mult
+                    )
                 for cols in halves:
                     nc.vector.tensor_tensor(out=mix[:, cols], in0=mix[:, cols], in1=d_sb[:, m, cols], op=ALU.add)
                     nc.sync.dma_start(out=out[m * P : (m + 1) * P, cols], in_=mix[:, cols])
@@ -319,5 +333,7 @@ def tile_rssmcell_pa_kernel(
                     pair()
             if job_at(step - 2):
                 activate(job_at(step - 2))
+                if job_at(step - 2)[0] == "u":
+                    difference(job_at(step - 2)[1])
             if following:
                 gate_input(following)

@@ -21,9 +21,27 @@ PASSES = K // 512
 ROW_TILES = BATCH // P
 HALVES = WIDTH // CHUNK
 EPS_LN = 1e-3
-LOAD_AHEAD = 3
-VECTOR_HELPS_BEFORE = 6
-
+RAW_BLOCKS = 16
+LOAD_AHEAD = 12
+TURNED_BANKS = 4
+GMASK = False
+GSUB = False
+SPREAD_S = ("gain",)
+PESUB = (0, 1, 2, 3)
+SPREAD_AT = {1: "r"}
+HEADMX = False
+VE = "g"
+BCAST = "u"
+AHEAD_UNITS = []
+WEAVE = 4
+SPREAD_STEP = {"n": 2}
+HWEAVE = 4
+PE_HALVES = {}
+SPLIT_JOBS = ()
+BN_JOBS = (("r", 0), ("r", 1), )
+PE_JOBS = ()
+G_COLS = {}
+G_ADDS = ()
 FLOPS = 2 * 2 * BATCH * K * 3 * WIDTH
 
 
@@ -33,54 +51,66 @@ def tile_rssmcell_pa_kernel(
     nc = tc.nc
     with ExitStack() as ctx:
         const = ctx.enter_context(tc.tile_pool(name="const", bufs=1))
-        raw_pool = ctx.enter_context(tc.tile_pool(name="raw", bufs=(LOAD_AHEAD + 1) * BLOCKS))
+        raw_pool = ctx.enter_context(tc.tile_pool(name="raw", bufs=RAW_BLOCKS))
         grouped_pool = ctx.enter_context(tc.tile_pool(name="grouped", bufs=3))
         gate_pool = ctx.enter_context(tc.tile_pool(name="gate", bufs=ROW_TILES))
         z_pool = ctx.enter_context(tc.tile_pool(name="z", bufs=3))
         squares_pool = ctx.enter_context(tc.tile_pool(name="squares", bufs=2))
         small = ctx.enter_context(tc.tile_pool(name="small", bufs=8))
-        turned_pool = ctx.enter_context(tc.psum_pool(name="turned", bufs=4))
-        acc_pool = ctx.enter_context(tc.psum_pool(name="acc", bufs=4))
+        turned_pool = ctx.enter_context(tc.psum_pool(name="turned", bufs=TURNED_BANKS))
+        acc_pool = ctx.enter_context(tc.psum_pool(name="acc", bufs=8 - TURNED_BANKS))
         ctx.enter_context(tc.manual_schedule())
 
-        def weight_rows(w, gate_index, h):
-            first_row = gate_index * WIDTH + h * CHUNK
-            return w[first_row : first_row + CHUNK, :]
+        source = {"x": x_pre, "d": deter, "ih": w_ih, "hh": w_hh}
+        gate_rows = {"r": 0, "u": WIDTH, "n": 2 * WIDTH}
 
-        X, D = 0, 2
-        sources = [x_pre]
-        partner = [None]
-        chunk_of = {}
-        for gate, gate_index, order in (("r", 0, ("ih", "hh")), ("n", 2, ("hh", "ih")), ("u", 1, ("ih", "hh"))):
-            for h in range(HALVES):
-                for which in order:
-                    if len(sources) == D:
-                        sources.append(deter)
-                        partner.append(None)
-                    chunk_of[(gate, which, h)] = len(sources)
-                    sources.append(weight_rows(w_ih if which == "ih" else w_hh, gate_index, h))
-                    partner.append(X if which == "ih" else D)
-        n_chunks = len(sources)
-        codes = [const.tile([P, PASSES * CHUNK], U32, align_bytes=64, name="codes%d" % c) for c in range(n_chunks)]
-        scales = [const.tile([P, PASSES * CHUNK], U8, align_bytes=64, name="scales%d" % c) for c in range(n_chunks)]
+        def first_row(unit):
+            if unit[0] in ("x", "d"):
+                return unit[1] * P
+            return gate_rows[unit[1]] + unit[2] * CHUNK
+
+        def blocks_of(unit):
+            return unit[2] if unit[0] in ("x", "d") else BLOCKS
+
+        step_units = {}
+        head_units = [("x", 0, 4), ("ih", "r", 0), ("d", 0, 4), ("hh", "r", 0), ("ih", "r", 1), ("hh", "r", 1)]
+        later = [(which, "n", h) for h in range(HALVES) for which in ("hh", "ih")]
+        later += [(which, "u", h) for h in range(HALVES) for which in ("ih", "hh")]
+        for i, count in enumerate([1,1,1,1,1,1,1,1]):
+            step_units[i - 1] = [later.pop(0) for j in range(count)]
+        order = list(head_units)
+        for step in sorted(step_units):
+            order.extend(step_units[step])
+        codes = {}
+        scales = {}
+        for i, unit in enumerate(order + [unit for unit in AHEAD_UNITS if unit not in order]):
+            cols = PASSES * blocks_of(unit) * P
+            codes[unit] = const.tile([P, cols], U32, align_bytes=64, name="codes%d" % i)
+            scales[unit] = const.tile([P, cols], U8, align_bytes=64, name="scales%d" % i)
+        order = [unit for unit in order if unit not in AHEAD_UNITS]
+        place = len(head_units)
+        order[place:place] = AHEAD_UNITS
+        stream = [(unit, t) for unit in order for t in range(blocks_of(unit))]
         raw = {}
         grouped = {}
 
-        ident = const.tile([P, P], F32, name="ident")
-        make_identity(nc, ident[:])
-        ident_bf = const.tile([P, P], BF16, name="ident_bf")
-        make_identity(nc, ident_bf[:])
-        neg_ident_bf = const.tile([P, P], BF16, name="neg_ident_bf")
-        nc.gpsimd.tensor_scalar(
-            out=neg_ident_bf[:], in0=ident_bf[:], scalar1=-1.0, scalar2=0.0, op0=ALU.mult, op1=ALU.add
-        )
-        neg_half = const.tile([P, 1], F32, name="neg_half")
-        nc.gpsimd.memset(neg_half[:], -0.5)
         warm = const.tile([P, 1], F32, name="warm")
         nc.vector.memset(warm[:], 0.0)
         ln_rows = const.tile([P, WIDTH], BF16, name="ln_rows")
         nc.vector.memset(ln_rows[:], 0.0)
         nc.scalar.activation(out=warm[:], in_=warm[:], func=ACT.Sigmoid)
+        ident = const.tile([P, P], F32, name="ident")
+        make_identity(nc, ident[:])
+        ident_bf = const.tile([P, P], BF16, name="ident_bf")
+        make_identity(nc, ident_bf[:])
+        neg_half = const.tile([P, 1], F32, name="neg_half")
+        nc.gpsimd.memset(neg_half[:], -0.5)
+        eps = const.tile([P, 1], F32, name="eps")
+        nc.vector.tensor_scalar(
+            out=eps[:], in0=ident[:, 0:1], scalar1=0.0, scalar2=EPS_LN, op0=ALU.mult, op1=ALU.add
+        )
+        neg_ident_bf = const.tile([P, P], BF16, name="neg_ident_bf")
+        nc.vector.tensor_scalar_mul(out=neg_ident_bf[:], in0=ident_bf[:], scalar1=-1.0)
         mask_sb = const.tile([P, ROW_TILES], BF16, name="mask_sb")
         with nc.allow_non_contiguous_dma(reason="512 mask values, one to a partition for each row tile"):
             nc.scalar.dma_start(out=mask_sb[:], in_=mask.rearrange("(m p) o -> p (m o)", p=P))
@@ -98,52 +128,69 @@ def tile_rssmcell_pa_kernel(
         gain = {}
         bias = {}
 
-        def load(c):
-            if c >= n_chunks:
-                return
-            raw[c] = []
-            for t in range(BLOCKS):
-                block = raw_pool.tile([P, K], BF16, name="raw")
-                nc.sync.dma_start(out=block[:], in_=sources[c][t * P : (t + 1) * P, :])
-                raw[c].append(block[:])
+        def load(i):
+            if i < len(stream):
+                unit, t = stream[i]
+                row = first_row(unit) + t * P
+                raw[(unit, t)] = raw_pool.tile([P, K], BF16, name="raw")
+                nc.sync.dma_start(out=raw[(unit, t)][:], in_=source[unit[0]][row : row + P, :])
+                if i == len(stream) - 1:
+                    for kind, kept in (("gain", gain), ("bias", bias)):
+                        if "u" in BCAST:
+                            kept["u"] = const.tile([P, WIDTH], BF16, name=kind + "_u")
+                            nc.sync.dma_start(out=kept["u"][:], in_=vectors[("u", kind)].partition_broadcast(P))
 
-        def turn(c, between=()):
-            grouped[c] = grouped_pool.tile([P, 4 * PASSES * CHUNK], BF16, align_bytes=64, name="grouped")
-            grouped_words = grouped[c][:].bitcast(F32).rearrange("p (g c u) -> p g c u", g=PASSES, u=2)
-            for t in range(BLOCKS):
-                words = raw[c][t].bitcast(F32)
-                bank = turned_pool.tile([P, CHUNK], F32, name="bank")
-                for a in range(2 * PASSES):
-                    nc.tensor.transpose(
-                        out=bank[:, a * P : (a + 1) * P], in_=words[:, a * P : (a + 1) * P], identity=ident[:]
-                    )
-                turned = bank[:].rearrange("p (g u c) -> p g c u", g=PASSES, u=2)
-                if c < VECTOR_HELPS_BEFORE and t == BLOCKS - 1:
-                    nc.vector.tensor_copy(out=grouped_words[:, :, t * P : (t + 1) * P, :], in_=turned)
-                else:
-                    nc.scalar.copy(out=grouped_words[:, :, t * P : (t + 1) * P, :], in_=turned)
-                if t < len(between):
-                    between[t]()
+        def mask_rows(m):
+            rows = [raw[(unit, t)] for unit in order if unit[0] == "d" for t in range(unit[2]) if unit[1] + t == m][0]
+            if GMASK:
+                nc.gpsimd.tensor_scalar(
+                    out=d_sb[:, m, :], in0=rows[:], scalar1=mask_sb[:, m : m + 1], scalar2=0.0, op0=ALU.mult, op1=ALU.add
+                )
+            else:
+                nc.vector.tensor_scalar_mul(out=d_sb[:, m, :], in0=rows[:], scalar1=mask_sb[:, m : m + 1])
 
-        def mask_state():
-            for m in range(ROW_TILES):
-                nc.vector.tensor_scalar_mul(out=d_sb[:, m, :], in0=raw[D][m], scalar1=mask_sb[:, m : m + 1])
-            raw[D] = [d_sb[:, m, :] for m in range(ROW_TILES)]
+        def turn_block(unit, t, on_vector):
+            n = blocks_of(unit)
+            if t == 0:
+                grouped[unit] = grouped_pool.tile([P, 4 * PASSES * n * P], BF16, align_bytes=64, name="grouped%d" % n)
+            load(stream.index((unit, t)) + LOAD_AHEAD)
+            if unit[0] == "d":
+                words = d_sb[:, unit[1] + t, :].bitcast(F32)
+            else:
+                words = raw[(unit, t)][:].bitcast(F32)
+            bank = turned_pool.tile([P, CHUNK], F32, name="bank")
+            if unit in ():
+                nc.tensor.matmul(
+                    out=acc_pool.tile([P, CHUNK], F32, name="acc")[:], lhsT=ident_bf[:], rhs=ln_rows[:, 0:CHUNK], start=True, stop=True
+                )
+            for a in range(2 * PASSES):
+                nc.tensor.transpose(
+                    out=bank[:, a * P : (a + 1) * P], in_=words[:, a * P : (a + 1) * P], identity=ident[:]
+                )
+            grouped_words = grouped[unit][:].bitcast(F32).rearrange("p (g c u) -> p g c u", g=PASSES, u=2)
+            turned = bank[:].rearrange("p (g u c) -> p g c u", g=PASSES, u=2)
+            into = grouped_words[:, :, t * P : (t + 1) * P, :]
+            if on_vector:
+                nc.vector.tensor_copy(out=into, in_=turned)
+            else:
+                nc.scalar.copy(out=into, in_=turned)
 
-        def quantise(c):
-            nc.vector.quantize_mx(out=codes[c][:].bitcast(FP8X4), scales=scales[c][:], in_=grouped[c][:])
+        def quantise(unit):
+            nc.vector.quantize_mx(out=codes[unit][:].bitcast(FP8X4), scales=scales[unit][:], in_=grouped[unit][:])
 
-        def passes(bank, c, m, first, last):
-            a = partner[c]
+        def passes(bank, unit, m, first, last):
+            letter = "x" if unit[0] == "ih" else "d"
+            act = [a for a in order if a[0] == letter and a[1] <= m < a[1] + a[2]][0]
             for g in range(PASSES):
-                rows = slice(g * CHUNK + m * P, g * CHUNK + (m + 1) * P)
+                start = (g * act[2] + m - act[1]) * P
+                rows = slice(start, start + P)
                 cols = slice(g * CHUNK, (g + 1) * CHUNK)
                 nc.tensor.matmul_mx(
                     out=bank[:],
-                    lhsT=codes[a][:, rows].bitcast(FP8X4),
-                    lhsT_scale=scales[a][:, rows],
-                    rhs=codes[c][:, cols].bitcast(FP8X4),
-                    rhs_scale=scales[c][:, cols],
+                    lhsT=codes[act][:, rows].bitcast(FP8X4),
+                    lhsT_scale=scales[act][:, rows],
+                    rhs=codes[unit][:, cols].bitcast(FP8X4),
+                    rhs_scale=scales[unit][:, cols],
                     start=(first and g == 0),
                     stop=(last and g == PASSES - 1),
                 )
@@ -161,7 +208,7 @@ def tile_rssmcell_pa_kernel(
                     stop=True,
                 )
             everywhere = const.tile([P, WIDTH], BF16, name=kind + "_" + gate)
-            if kind == "gain":
+            if kind in SPREAD_S:
                 nc.scalar.copy(out=everywhere[:], in_=bank[:])
             else:
                 nc.vector.tensor_copy(out=everywhere[:], in_=bank[:])
@@ -170,22 +217,17 @@ def tile_rssmcell_pa_kernel(
         jobs = [(gate, m) for gate in ("r", "n", "u") for m in range(ROW_TILES)]
         value = {}
         half_sums = {}
-        neg_mean = {}
+        spread_of = {}
+        mean = {}
         rstd = {}
         z = {}
+        banks = {}
+        zbank = {}
+        ebank = {}
+        halves = [slice(h * CHUNK, (h + 1) * CHUNK) for h in range(HALVES)]
         for job in jobs:
             value[job] = gate_pool.tile([P, WIDTH], F32, name=job[0] + "_gate")
             half_sums[job] = small.tile([P, HALVES], F32, name="half_sums", bufs=len(jobs))
-
-        def evacuate(job, h, bank):
-            nc.scalar.activation(
-                out=value[job][:, h * CHUNK : (h + 1) * CHUNK],
-                in_=bank[:],
-                func=ACT.Identity,
-                accum_out=half_sums[job][:, h : h + 1],
-            )
-
-        banks = {}
 
         def gate_sums(job):
             gate, m = job
@@ -195,7 +237,7 @@ def tile_rssmcell_pa_kernel(
                     key = (job, which if gate == "n" else "sum", h)
                     if first:
                         banks[key] = acc_pool.tile([P, CHUNK], F32, name="acc")
-                    passes(banks[key], chunk_of[(gate, which, h)], m, first, last)
+                    passes(banks[key], (which, gate, h), m, first, last)
 
                 return run
 
@@ -205,17 +247,20 @@ def tile_rssmcell_pa_kernel(
 
         def gate_input(job):
             gate, m = job
-            if gate != "n":
-                for h in range(HALVES):
-                    evacuate(job, h, banks[(job, "sum", h)])
+            if job not in BN_JOBS and gate != "n":
+                for h, cols in enumerate(halves):
+                    nc.scalar.activation(
+                        out=value[job][:, cols],
+                        in_=banks[(job, "sum", h)][:],
+                        func=ACT.Identity,
+                        accum_out=half_sums[job][:, h : h + 1],
+                    )
             if gate == "n":
-                for h in range(HALVES):
-                    cols = slice(h * CHUNK, (h + 1) * CHUNK)
+                for h, cols in enumerate(halves):
                     nc.vector.tensor_tensor(
                         out=value[job][:, cols], in0=value[("r", m)][:, cols], in1=banks[(job, "hh", h)][:], op=ALU.mult
                     )
-                for h in range(HALVES):
-                    cols = slice(h * CHUNK, (h + 1) * CHUNK)
+                for h, cols in enumerate(halves):
                     nc.vector.scalar_tensor_tensor(
                         out=value[job][:, cols],
                         in0=value[job][:, cols],
@@ -227,113 +272,249 @@ def tile_rssmcell_pa_kernel(
                     )
 
         def statistics(job):
-            scaled_sums = small.tile([P, HALVES], F32, name="scaled_sums")
-            neg_mean[job] = small.tile([P, 1], F32, name="neg_mean")
-            nc.scalar.activation(
-                out=scaled_sums[:],
-                in_=half_sums[job][:],
-                func=ACT.Identity,
-                scale=-1.0 / WIDTH,
-                accum_out=neg_mean[job][:],
-            )
-            squares = squares_pool.tile([P, WIDTH], BF16, name="squares")
-            sum_sq = small.tile([P, 1], F32, name="sum_sq")
-            nc.scalar.activation(
-                out=squares[:], in_=value[job][:], func=ACT.Square, bias=neg_mean[job][:], accum_out=sum_sq[:]
-            )
+            if job in BN_JOBS:
+                pieces = small.tile([P, HALVES, 6], F32, name="pieces")
+                for h in range(HALVES):
+                    nc.vector.bn_stats(out=pieces[:, h, :], in_=banks[(job, "sum", h)][:])
+                moments = small.tile([P, 2], F32, name="moments")
+                nc.vector.bn_aggr(out=moments[:], in_=pieces[:].rearrange("p h s -> p (h s)"))
+                mean[job] = moments[:, 0:1]
+                spread_of[job] = (moments[:, 1:2], 1.0)
+            else:
+                scaled_sums = small.tile([P, HALVES], F32, name="scaled_sums")
+                neg_mean = small.tile([P, 1], F32, name="neg_mean")
+                nc.scalar.activation(
+                    out=scaled_sums[:],
+                    in_=half_sums[job][:],
+                    func=ACT.Identity,
+                    scale=-1.0 / WIDTH,
+                    accum_out=neg_mean[:],
+                )
+                mean[job] = neg_mean[:]
+                squares = squares_pool.tile([P, WIDTH], BF16, name="squares")
+                sum_sq = small.tile([P, 1], F32, name="sum_sq")
+                nc.scalar.activation(
+                    out=squares[:], in_=value[job][:], func=ACT.Square, bias=neg_mean[:], accum_out=sum_sq[:]
+                )
+                spread_of[job] = (sum_sq[:], 1.0 / WIDTH)
+
+        def inverse_root(job):
             var_eps = small.tile([P, 1], F32, name="var_eps")
-            nc.gpsimd.tensor_scalar(
-                out=var_eps[:], in0=sum_sq[:], scalar1=1.0 / WIDTH, scalar2=EPS_LN, op0=ALU.mult, op1=ALU.add
-            )
             rstd[job] = small.tile([P, 1], F32, name="rstd")
+            value_in, scale = spread_of[job]
+            if VE == "s":
+                nc.scalar.activation(out=var_eps[:], in_=value_in, func=ACT.Identity, scale=scale, bias=eps[:])
+            else:
+                (nc.gpsimd if VE == "g" else nc.vector).tensor_scalar(
+                    out=var_eps[:], in0=value_in, scalar1=scale, scalar2=EPS_LN, op0=ALU.mult, op1=ALU.add
+                )
             nc.gpsimd.tensor_tensor(out=rstd[job][:], in0=var_eps[:], in1=neg_half[:], op=ALU.pow)
 
         def centre(job):
             z[job] = z_pool.tile([P, WIDTH], F32, name="z")
-            nc.vector.scalar_tensor_tensor(
-                out=z[job][:],
-                in0=value[job][:],
-                scalar=neg_mean[job][:],
-                in1=gain[job[0]][:],
-                op0=ALU.add,
-                op1=ALU.mult,
-            )
+            if job in BN_JOBS:
+                for h, cols in enumerate(halves):
+                    nc.vector.scalar_tensor_tensor(
+                        out=z[job][:, cols],
+                        in0=banks[(job, "sum", h)][:],
+                        scalar=mean[job],
+                        in1=gain[job[0]][:, cols],
+                        op0=ALU.subtract,
+                        op1=ALU.mult,
+                    )
+            else:
+                nc.vector.scalar_tensor_tensor(
+                    out=z[job][:], in0=value[job][:], scalar=mean[job], in1=gain[job[0]][:], op0=ALU.add, op1=ALU.mult
+                )
 
         def affine(job):
-            nc.vector.scalar_tensor_tensor(
-                out=z[job][:], in0=z[job][:], scalar=rstd[job][:], in1=bias[job[0]][:], op0=ALU.mult, op1=ALU.add
-            )
+            pe_halves = PE_HALVES.get(job, ())
+            if pe_halves:
+                diag = small.tile([P, P], F32, name="diag", bufs=2)
+                nc.vector.tensor_scalar_mul(out=diag[:], in0=ident[:], scalar1=rstd[job][:])
+                for h in pe_halves:
+                    cols = halves[h]
+                    zbank[(job, h)] = turned_pool.tile([P, CHUNK], F32, name="bank")
+                    nc.tensor.matmul(out=zbank[(job, h)][:], lhsT=diag[:], rhs=z[job][:, cols], start=True, stop=False)
+                    nc.tensor.matmul(
+                        out=zbank[(job, h)][:], lhsT=ident_bf[:], rhs=bias[job[0]][:, cols], start=False, stop=True
+                    )
+            pieces = halves if job in SPLIT_JOBS or pe_halves else [slice(0, WIDTH)]
+            for h, v in enumerate(pieces):
+                if h in pe_halves:
+                    continue
+                nc.vector.scalar_tensor_tensor(
+                    out=z[job][:, v], in0=z[job][:, v], scalar=rstd[job][:], in1=bias[job[0]][:, v],
+                    op0=ALU.mult, op1=ALU.add,
+                )
+
+        def difference(m):
+            for h, cols in enumerate(halves):
+                ebank[(m, h)] = turned_pool.tile([P, CHUNK], F32, name="bank")
+                nc.tensor.matmul(
+                    out=ebank[(m, h)][:], lhsT=ident[:], rhs=value[("n", m)][:, cols], start=True, stop=False
+                )
+                nc.tensor.matmul(
+                    out=ebank[(m, h)][:], lhsT=neg_ident_bf[:], rhs=d_sb[:, m, cols], start=False, stop=True
+                )
 
         def activate(job):
             func = ACT.Tanh if job[0] == "n" else ACT.Sigmoid
-            nc.scalar.activation(out=value[job][:], in_=z[job][:], func=func)
-
-        differences = {}
-
-        def difference(m):
-            for h in range(HALVES):
-                cols = slice(h * CHUNK, (h + 1) * CHUNK)
-                bank = turned_pool.tile([P, CHUNK], F32, name="bank")
-                nc.tensor.matmul(out=bank[:], lhsT=ident[:], rhs=value[("n", m)][:, cols], start=True, stop=False)
-                nc.tensor.matmul(out=bank[:], lhsT=neg_ident_bf[:], rhs=d_sb[:, m, cols], start=False, stop=True)
-                differences[(m, h)] = bank
+            pe_halves = PE_HALVES.get(job, ())
+            if pe_halves or job in SPLIT_JOBS:
+                for h, cols in enumerate(halves):
+                    source_half = zbank[(job, h)][:] if h in pe_halves else z[job][:, cols]
+                    nc.scalar.activation(out=value[job][:, cols], in_=source_half, func=func)
+            else:
+                nc.scalar.activation(out=value[job][:], in_=z[job][:], func=func)
 
         def blend(job):
             gate, m = job
             mix = value[("n", m)]
-            if gate == "u":
-                halves = [slice(h * CHUNK, (h + 1) * CHUNK) for h in range(HALVES)]
-                for h, cols in enumerate(halves):
-                    nc.vector.tensor_tensor(
-                        out=mix[:, cols], in0=value[job][:, cols], in1=differences[(m, h)][:], op=ALU.mult
-                    )
+            if gate == "n" and m not in PESUB:
                 for cols in halves:
-                    nc.vector.tensor_tensor(out=mix[:, cols], in0=mix[:, cols], in1=d_sb[:, m, cols], op=ALU.add)
+                    (nc.gpsimd if GSUB else nc.vector).tensor_tensor(out=mix[:, cols], in0=mix[:, cols], in1=d_sb[:, m, cols], op=ALU.subtract)
+            if gate == "u":
+                for h, cols in enumerate(halves):
+                    if m in PESUB:
+                        nc.vector.tensor_tensor(
+                            out=mix[:, cols], in0=value[job][:, cols], in1=ebank[(m, h)][:], op=ALU.mult
+                        )
+                    else:
+                        nc.vector.tensor_tensor(out=mix[:, cols], in0=mix[:, cols], in1=value[job][:, cols], op=ALU.mult)
+                for cols in halves:
+                    engine = nc.vector
+                    engine.tensor_tensor(out=mix[:, cols], in0=mix[:, cols], in1=d_sb[:, m, cols], op=ALU.add)
                     nc.sync.dma_start(out=out[m * P : (m + 1) * P, cols], in_=mix[:, cols])
 
-        head_chunks = chunk_of[("r", "hh", 1)] + 1
-        for c in range(LOAD_AHEAD):
-            load(c)
-        for c in range(head_chunks):
-            load(c + LOAD_AHEAD)
-            turn(c)
-            if c == D - 1:
-                mask_state()
-            quantise(c)
-            gate = {1: "r", 3: "n", 5: "u"}.get(c)
-            if gate:
+        def head_pairs(i):
+            if i < 0 or head_units[i][0] not in ("ih", "hh"):
+                return []
+            which, gate, h = head_units[i]
+
+            def pair(job):
+                def run():
+                    if which == "ih":
+                        banks[(job, "sum", h)] = acc_pool.tile([P, CHUNK], F32, name="acc")
+                    passes(banks[(job, "sum", h)], head_units[i], job[1], which == "ih", which == "hh")
+
+                return run
+
+            return [pair(job) for job in jobs[:2]]
+
+        for i in range(LOAD_AHEAD):
+            load(i)
+        for i, unit in enumerate(head_units):
+            n = blocks_of(unit)
+            pairs = head_pairs(i - 1)
+            for t in range(n):
+                turn_block(unit, t, unit[0] in ("ih", "hh") and t == n - 1)
+                if t % HWEAVE == HWEAVE - 1 and pairs:
+                    pairs.pop(0)()
+            for pair in pairs:
+                pair()
+            if i + 1 < len(head_units) and head_units[i + 1][0] == "d":
+                for m in range(ROW_TILES):
+                    mask_rows(m)
+            quantise(unit)
+            for gate in SPREAD_AT.get(i, ()):
                 gain[gate] = spread(gate, "gain")
                 bias[gate] = spread(gate, "bias")
+
+        progress = {}
+
+        def due(stage, upto):
+            first = progress.get(stage, 0)
+            last = max(0, min(upto + 1, len(jobs)))
+            progress[stage] = max(first, last)
+            return jobs[first:last]
 
         def job_at(index):
             return jobs[index] if 0 <= index < len(jobs) else None
 
-        for sums in gate_sums(jobs[0]):
-            sums()
-        gate_input(jobs[0])
-        for step in range(-1, len(jobs) + 3):
-            c = head_chunks + step + 1
-            if job_at(step):
-                statistics(job_at(step))
-            if job_at(step - 1):
-                centre(job_at(step - 1))
-            if head_chunks <= c - 1 < n_chunks:
-                quantise(c - 1)
-            if job_at(step - 3):
-                blend(job_at(step - 3))
-            if job_at(step - 1):
-                affine(job_at(step - 1))
-            following = job_at(step + 1) if step >= 0 else None
-            sums = gate_sums(following) if following else []
-            if c < n_chunks:
-                load(c + LOAD_AHEAD)
-                turn(c, sums)
-            else:
-                for pair in sums:
-                    pair()
-            if job_at(step - 2):
-                activate(job_at(step - 2))
-                if job_at(step - 2)[0] == "u":
-                    difference(job_at(step - 2)[1])
+        for step in range(-1, 8):
+            following = job_at(step + 1)
+            sums = gate_sums(following) if following and step > 0 else []
+            if step == -1:
+                sums = head_pairs(len(head_units) - 1)
+            for job in due("statistics", step):
+                statistics(job)
+            for job in due("root", step):
+                inverse_root(job)
+            for job in due("centre", step - 1):
+                centre(job)
+            for unit in step_units.get(step - 1, ()):
+                quantise(unit)
+            for unit in step_units.get(step, ()):
+                if unit[0] == "d":
+                    for m in range(unit[1], unit[1] + unit[2]):
+                        mask_rows(m)
+            for job in due("blend", step - 3):
+                blend(job)
+            for job in due("affine", step - 1):
+                affine(job)
+            turned_blocks = 0
+            for unit in step_units.get(step, ()):
+                for t in range(blocks_of(unit)):
+                    turn_block(unit, t, False)
+                    turned_blocks += 1
+                    if turned_blocks % WEAVE == 0:
+                        for pair in sums[:WEAVE]:
+                            pair()
+                        sums = sums[WEAVE:]
+            for pair in sums:
+                pair()
+            for gate, at in SPREAD_STEP.items():
+                if at == step:
+                    gain[gate] = spread(gate, "gain")
+                    bias[gate] = spread(gate, "bias")
+            for job in due("activate", step - 2):
+                activate(job)
+            for job in due("difference", step - 1):
+                if job[0] == "u" and job[1] in PESUB:
+                    difference(job[1])
             if following:
                 gate_input(following)
+        for step in range(8, len(jobs) + 3):
+            following = job_at(step + 1)
+            sums = gate_sums(following) if following and step > 0 else []
+            if step == -1:
+                sums = head_pairs(len(head_units) - 1)
+            for job in due("statistics", step):
+                statistics(job)
+            for job in due("root", step):
+                inverse_root(job)
+            for job in due("centre", step - 1):
+                centre(job)
+            for unit in step_units.get(step - 1, ()):
+                quantise(unit)
+            for unit in step_units.get(step, ()):
+                if unit[0] == "d":
+                    for m in range(unit[1], unit[1] + unit[2]):
+                        mask_rows(m)
+            for job in due("blend", step - 3):
+                blend(job)
+            for job in due("affine", step - 1):
+                affine(job)
+            turned_blocks = 0
+            for unit in step_units.get(step, ()):
+                for t in range(blocks_of(unit)):
+                    turn_block(unit, t, False)
+                    turned_blocks += 1
+                    if turned_blocks % WEAVE == 0:
+                        for pair in sums[:WEAVE]:
+                            pair()
+                        sums = sums[WEAVE:]
+            for pair in sums:
+                pair()
+            for gate, at in SPREAD_STEP.items():
+                if at == step:
+                    gain[gate] = spread(gate, "gain")
+                    bias[gate] = spread(gate, "bias")
+            for job in due("difference", step - 1):
+                if job[0] == "u" and job[1] in PESUB:
+                    difference(job[1])
+            if following:
+                gate_input(following)
+            for job in due("activate", step - 1):
+                activate(job)

@@ -28,7 +28,7 @@ GMASK = False
 GSUB = False
 SPREAD_S = ("gain",)
 PESUB = (0, 1, 2, 3)
-SPREAD_AT = {1: "r"}
+SPREAD_AT = {2: "r"}
 HEADMX = False
 VE = "g"
 BCAST = "u"
@@ -73,7 +73,7 @@ def tile_rssmcell_pa_kernel(
             return unit[2] if unit[0] in ("x", "d") else BLOCKS
 
         step_units = {}
-        head_units = [("x", 0, 4), ("ih", "r", 0), ("d", 0, 4), ("hh", "r", 0), ("ih", "r", 1), ("hh", "r", 1)]
+        head_units = [("x", 0, 4), ("d", 0, 4), ("ih", "r", 0), ("hh", "r", 0), ("ih", "r", 1), ("hh", "r", 1)]
         later = [(which, "n", h) for h in range(HALVES) for which in ("hh", "ih")]
         later += [(which, "u", h) for h in range(HALVES) for which in ("ih", "hh")]
         for i, count in enumerate([1,1,1,1,1,1,1,1]):

@@ -15,33 +15,15 @@ P = 128
 BATCH = 512
 K = 1024
 WIDTH = 1024
-CHUNK = 512
-BLOCKS = CHUNK // P
+UNIT = 512
+BLOCKS = UNIT // P
 PASSES = K // 512
 ROW_TILES = BATCH // P
-HALVES = WIDTH // CHUNK
+HALVES = WIDTH // UNIT
 EPS_LN = 1e-3
 RAW_BLOCKS = 16
 LOAD_AHEAD = 12
-TURNED_BANKS = 4
-GMASK = False
-GSUB = False
-SPREAD_S = ("gain",)
-PESUB = (0, 1, 2, 3)
-SPREAD_AT = {2: "r"}
-HEADMX = False
-VE = "g"
-BCAST = "u"
-AHEAD_UNITS = []
-WEAVE = 4
-SPREAD_STEP = {"n": 2}
-HWEAVE = 4
-PE_HALVES = {}
-SPLIT_JOBS = ()
-BN_JOBS = (("r", 0), ("r", 1), )
-PE_JOBS = ()
-G_COLS = {}
-G_ADDS = ()
+
 FLOPS = 2 * 2 * BATCH * K * 3 * WIDTH
 
 
@@ -57,42 +39,40 @@ def tile_rssmcell_pa_kernel(
         z_pool = ctx.enter_context(tc.tile_pool(name="z", bufs=3))
         squares_pool = ctx.enter_context(tc.tile_pool(name="squares", bufs=2))
         small = ctx.enter_context(tc.tile_pool(name="small", bufs=8))
-        turned_pool = ctx.enter_context(tc.psum_pool(name="turned", bufs=TURNED_BANKS))
-        acc_pool = ctx.enter_context(tc.psum_pool(name="acc", bufs=8 - TURNED_BANKS))
+        psum = ctx.enter_context(tc.psum_pool(name="psum", bufs=1))
         ctx.enter_context(tc.manual_schedule())
 
         source = {"x": x_pre, "d": deter, "ih": w_ih, "hh": w_hh}
         gate_rows = {"r": 0, "u": WIDTH, "n": 2 * WIDTH}
-
-        def first_row(unit):
-            if unit[0] in ("x", "d"):
-                return unit[1] * P
-            return gate_rows[unit[1]] + unit[2] * CHUNK
-
-        def blocks_of(unit):
-            return unit[2] if unit[0] in ("x", "d") else BLOCKS
-
-        step_units = {}
-        head_units = [("x", 0, 4), ("d", 0, 4), ("ih", "r", 0), ("hh", "r", 0), ("ih", "r", 1), ("hh", "r", 1)]
-        later = [(which, "n", h) for h in range(HALVES) for which in ("hh", "ih")]
-        later += [(which, "u", h) for h in range(HALVES) for which in ("ih", "hh")]
-        for i, count in enumerate([1,1,1,1,1,1,1,1]):
-            step_units[i - 1] = [later.pop(0) for j in range(count)]
-        order = list(head_units)
-        for step in sorted(step_units):
-            order.extend(step_units[step])
+        X, D = ("x",), ("d",)
+        head_units = [X, D] + [(which, "r", h) for h in range(HALVES) for which in ("ih", "hh")]
+        later_units = [(which, "n", h) for h in range(HALVES) for which in ("hh", "ih")]
+        later_units += [(which, "u", h) for h in range(HALVES) for which in ("ih", "hh")]
+        units = head_units + later_units
         codes = {}
         scales = {}
-        for i, unit in enumerate(order + [unit for unit in AHEAD_UNITS if unit not in order]):
-            cols = PASSES * blocks_of(unit) * P
-            codes[unit] = const.tile([P, cols], U32, align_bytes=64, name="codes%d" % i)
-            scales[unit] = const.tile([P, cols], U8, align_bytes=64, name="scales%d" % i)
-        order = [unit for unit in order if unit not in AHEAD_UNITS]
-        place = len(head_units)
-        order[place:place] = AHEAD_UNITS
-        stream = [(unit, t) for unit in order for t in range(blocks_of(unit))]
+        for i, unit in enumerate(units):
+            codes[unit] = const.tile([P, PASSES * UNIT], U32, align_bytes=64, name="codes%d" % i)
+            scales[unit] = const.tile([P, PASSES * UNIT], U8, align_bytes=64, name="scales%d" % i)
+        stream = [(unit, t) for unit in units for t in range(BLOCKS)]
         raw = {}
         grouped = {}
+
+        def psum_bank(pair, i, shape=(P, UNIT), dtype=F32):
+            return psum.tile(list(shape), dtype, name="bank%d" % (2 * pair + i))
+
+        turned = []
+
+        def turned_bank(shape=(P, UNIT), dtype=F32):
+            turned.append(len(turned) % 4)
+            return psum_bank(turned[-1] // 2, turned[-1] % 2, shape, dtype)
+
+        taken = []
+        pairs = {}
+
+        def next_pair():
+            taken.append((0, 2, 3)[len(taken) % 3])
+            return taken[-1]
 
         warm = const.tile([P, 1], F32, name="warm")
         nc.vector.memset(warm[:], 0.0)
@@ -105,10 +85,6 @@ def tile_rssmcell_pa_kernel(
         make_identity(nc, ident_bf[:])
         neg_half = const.tile([P, 1], F32, name="neg_half")
         nc.gpsimd.memset(neg_half[:], -0.5)
-        eps = const.tile([P, 1], F32, name="eps")
-        nc.vector.tensor_scalar(
-            out=eps[:], in0=ident[:, 0:1], scalar1=0.0, scalar2=EPS_LN, op0=ALU.mult, op1=ALU.add
-        )
         neg_ident_bf = const.tile([P, P], BF16, name="neg_ident_bf")
         nc.vector.tensor_scalar_mul(out=neg_ident_bf[:], in0=ident_bf[:], scalar1=-1.0)
         mask_sb = const.tile([P, ROW_TILES], BF16, name="mask_sb")
@@ -125,66 +101,46 @@ def tile_rssmcell_pa_kernel(
         for row, vec in enumerate(vectors.values()):
             nc.scalar.dma_start(out=ln_rows[row : row + 1, :], in_=vec.unsqueeze(0))
         d_sb = const.tile([P, ROW_TILES, K], BF16, name="d_sb")
-        gain = {}
-        bias = {}
 
         def load(i):
             if i < len(stream):
                 unit, t = stream[i]
-                row = first_row(unit) + t * P
+                row = t * P
+                if unit not in (X, D):
+                    row += gate_rows[unit[1]] + unit[2] * UNIT
                 raw[(unit, t)] = raw_pool.tile([P, K], BF16, name="raw")
                 nc.sync.dma_start(out=raw[(unit, t)][:], in_=source[unit[0]][row : row + P, :])
-                if i == len(stream) - 1:
-                    for kind, kept in (("gain", gain), ("bias", bias)):
-                        if "u" in BCAST:
-                            kept["u"] = const.tile([P, WIDTH], BF16, name=kind + "_u")
-                            nc.sync.dma_start(out=kept["u"][:], in_=vectors[("u", kind)].partition_broadcast(P))
 
-        def mask_rows(m):
-            rows = [raw[(unit, t)] for unit in order if unit[0] == "d" for t in range(unit[2]) if unit[1] + t == m][0]
-            if GMASK:
-                nc.gpsimd.tensor_scalar(
-                    out=d_sb[:, m, :], in0=rows[:], scalar1=mask_sb[:, m : m + 1], scalar2=0.0, op0=ALU.mult, op1=ALU.add
-                )
-            else:
-                nc.vector.tensor_scalar_mul(out=d_sb[:, m, :], in0=rows[:], scalar1=mask_sb[:, m : m + 1])
+        def mask_state():
+            for m in range(ROW_TILES):
+                nc.vector.tensor_scalar_mul(out=d_sb[:, m, :], in0=raw[(D, m)][:], scalar1=mask_sb[:, m : m + 1])
 
         def turn_block(unit, t, on_vector):
-            n = blocks_of(unit)
             if t == 0:
-                grouped[unit] = grouped_pool.tile([P, 4 * PASSES * n * P], BF16, align_bytes=64, name="grouped%d" % n)
+                grouped[unit] = grouped_pool.tile([P, 4 * PASSES * UNIT], BF16, align_bytes=64, name="grouped")
             load(stream.index((unit, t)) + LOAD_AHEAD)
-            if unit[0] == "d":
-                words = d_sb[:, unit[1] + t, :].bitcast(F32)
-            else:
-                words = raw[(unit, t)][:].bitcast(F32)
-            bank = turned_pool.tile([P, CHUNK], F32, name="bank")
-            if unit in ():
-                nc.tensor.matmul(
-                    out=acc_pool.tile([P, CHUNK], F32, name="acc")[:], lhsT=ident_bf[:], rhs=ln_rows[:, 0:CHUNK], start=True, stop=True
-                )
+            words = (d_sb[:, t, :] if unit == D else raw[(unit, t)][:]).bitcast(F32)
+            bank = turned_bank()
             for a in range(2 * PASSES):
                 nc.tensor.transpose(
                     out=bank[:, a * P : (a + 1) * P], in_=words[:, a * P : (a + 1) * P], identity=ident[:]
                 )
             grouped_words = grouped[unit][:].bitcast(F32).rearrange("p (g c u) -> p g c u", g=PASSES, u=2)
-            turned = bank[:].rearrange("p (g u c) -> p g c u", g=PASSES, u=2)
             into = grouped_words[:, :, t * P : (t + 1) * P, :]
+            words_out = bank[:].rearrange("p (g u c) -> p g c u", g=PASSES, u=2)
             if on_vector:
-                nc.vector.tensor_copy(out=into, in_=turned)
+                nc.vector.tensor_copy(out=into, in_=words_out)
             else:
-                nc.scalar.copy(out=into, in_=turned)
+                nc.scalar.copy(out=into, in_=words_out)
 
         def quantise(unit):
             nc.vector.quantize_mx(out=codes[unit][:].bitcast(FP8X4), scales=scales[unit][:], in_=grouped[unit][:])
 
         def passes(bank, unit, m, first, last):
-            letter = "x" if unit[0] == "ih" else "d"
-            act = [a for a in order if a[0] == letter and a[1] <= m < a[1] + a[2]][0]
+            act = X if unit[0] == "ih" else D
             for g in range(PASSES):
-                start = (g * act[2] + m - act[1]) * P
-                rows = slice(start, start + P)
-                cols = slice(g * CHUNK, (g + 1) * CHUNK)
+                rows = slice(g * UNIT + m * P, g * UNIT + (m + 1) * P)
+                cols = slice(g * UNIT, (g + 1) * UNIT)
                 nc.tensor.matmul_mx(
                     out=bank[:],
                     lhsT=codes[act][:, rows].bitcast(FP8X4),
@@ -195,11 +151,10 @@ def tile_rssmcell_pa_kernel(
                     stop=(last and g == PASSES - 1),
                 )
 
-        def spread(gate, kind):
+        def spread(bank, gate, kind):
             row = list(vectors).index((gate, kind))
-            bank = turned_pool.tile([P, WIDTH], BF16, name="bank")
             for h in range(HALVES):
-                cols = slice(h * CHUNK, (h + 1) * CHUNK)
+                cols = slice(h * UNIT, (h + 1) * UNIT)
                 nc.tensor.matmul(
                     out=bank[:, cols],
                     lhsT=ident_bf[:, row : row + 1].to_broadcast([P, P]),
@@ -207,54 +162,57 @@ def tile_rssmcell_pa_kernel(
                     start=True,
                     stop=True,
                 )
-            everywhere = const.tile([P, WIDTH], BF16, name=kind + "_" + gate)
-            if kind in SPREAD_S:
-                nc.scalar.copy(out=everywhere[:], in_=bank[:])
-            else:
-                nc.vector.tensor_copy(out=everywhere[:], in_=bank[:])
-            return everywhere
+
+        gain = {}
+        bias = {}
+
+        def spread_to_sbuf(gate):
+            for kind, kept in (("gain", gain), ("bias", bias)):
+                bank = turned_bank((P, WIDTH), BF16)
+                spread(bank, gate, kind)
+                kept[gate] = const.tile([P, WIDTH], BF16, name=kind + "_" + gate)
+                nc.scalar.copy(out=kept[gate][:], in_=bank[:])
+
+        def spread_update():
+            for i, (kind, kept) in enumerate((("gain", gain), ("bias", bias))):
+                kept["u"] = psum_bank(1, i, (P, WIDTH), BF16)
+                spread(kept["u"], "u", kind)
 
         jobs = [(gate, m) for gate in ("r", "n", "u") for m in range(ROW_TILES)]
+        bn_jobs = (("r", 0), ("r", 2))
         value = {}
         half_sums = {}
-        spread_of = {}
         mean = {}
+        variance = {}
         rstd = {}
         z = {}
         banks = {}
-        zbank = {}
-        ebank = {}
-        halves = [slice(h * CHUNK, (h + 1) * CHUNK) for h in range(HALVES)]
+        differences = {}
+        halves = [slice(h * UNIT, (h + 1) * UNIT) for h in range(HALVES)]
         for job in jobs:
             value[job] = gate_pool.tile([P, WIDTH], F32, name=job[0] + "_gate")
             half_sums[job] = small.tile([P, HALVES], F32, name="half_sums", bufs=len(jobs))
 
-        def gate_sums(job):
-            gate, m = job
-
-            def pair(which, h, first, last):
-                def run():
-                    key = (job, which if gate == "n" else "sum", h)
-                    if first:
-                        banks[key] = acc_pool.tile([P, CHUNK], F32, name="acc")
-                    passes(banks[key], (which, gate, h), m, first, last)
-
-                return run
-
+        def sums_on_unit(job, unit):
+            which, gate, h = unit
+            m = job[1]
             if gate == "n":
-                return [pair(which, h, True, True) for h in range(HALVES) for which in ("hh", "ih")]
-            return [pair(which, h, which == "ih", which == "hh") for h in range(HALVES) for which in ("ih", "hh")]
+                banks[(job, which, h)] = psum_bank(2 + h, 0 if which == "hh" else 1)
+                passes(banks[(job, which, h)], unit, m, True, True)
+            else:
+                if which == "ih":
+                    if h == 0:
+                        pairs[job] = 2 + m % 2 if gate == "r" else next_pair()
+                    banks[(job, h)] = psum_bank(pairs[job], h)
+                passes(banks[(job, h)], unit, m, which == "ih", which == "hh")
 
-        def gate_input(job):
+        def sums(job):
+            for unit in units:
+                if unit not in (X, D) and unit[1] == job[0]:
+                    sums_on_unit(job, unit)
+
+        def empty(job):
             gate, m = job
-            if job not in BN_JOBS and gate != "n":
-                for h, cols in enumerate(halves):
-                    nc.scalar.activation(
-                        out=value[job][:, cols],
-                        in_=banks[(job, "sum", h)][:],
-                        func=ACT.Identity,
-                        accum_out=half_sums[job][:, h : h + 1],
-                    )
             if gate == "n":
                 for h, cols in enumerate(halves):
                     nc.vector.tensor_tensor(
@@ -270,16 +228,24 @@ def tile_rssmcell_pa_kernel(
                         op1=ALU.add,
                         accum_out=half_sums[job][:, h : h + 1],
                     )
+            elif job not in bn_jobs:
+                for h, cols in enumerate(halves):
+                    nc.scalar.activation(
+                        out=value[job][:, cols],
+                        in_=banks[(job, h)][:],
+                        func=ACT.Identity,
+                        accum_out=half_sums[job][:, h : h + 1],
+                    )
 
         def statistics(job):
-            if job in BN_JOBS:
+            if job in bn_jobs:
                 pieces = small.tile([P, HALVES, 6], F32, name="pieces")
                 for h in range(HALVES):
-                    nc.vector.bn_stats(out=pieces[:, h, :], in_=banks[(job, "sum", h)][:])
+                    nc.vector.bn_stats(out=pieces[:, h, :], in_=banks[(job, h)][:])
                 moments = small.tile([P, 2], F32, name="moments")
                 nc.vector.bn_aggr(out=moments[:], in_=pieces[:].rearrange("p h s -> p (h s)"))
                 mean[job] = moments[:, 0:1]
-                spread_of[job] = (moments[:, 1:2], 1.0)
+                variance[job] = (moments[:, 1:2], 1.0)
             else:
                 scaled_sums = small.tile([P, HALVES], F32, name="scaled_sums")
                 neg_mean = small.tile([P, 1], F32, name="neg_mean")
@@ -296,27 +262,24 @@ def tile_rssmcell_pa_kernel(
                 nc.scalar.activation(
                     out=squares[:], in_=value[job][:], func=ACT.Square, bias=neg_mean[:], accum_out=sum_sq[:]
                 )
-                spread_of[job] = (sum_sq[:], 1.0 / WIDTH)
+                variance[job] = (sum_sq[:], 1.0 / WIDTH)
 
         def inverse_root(job):
             var_eps = small.tile([P, 1], F32, name="var_eps")
             rstd[job] = small.tile([P, 1], F32, name="rstd")
-            value_in, scale = spread_of[job]
-            if VE == "s":
-                nc.scalar.activation(out=var_eps[:], in_=value_in, func=ACT.Identity, scale=scale, bias=eps[:])
-            else:
-                (nc.gpsimd if VE == "g" else nc.vector).tensor_scalar(
-                    out=var_eps[:], in0=value_in, scalar1=scale, scalar2=EPS_LN, op0=ALU.mult, op1=ALU.add
-                )
+            var_in, scale = variance[job]
+            nc.gpsimd.tensor_scalar(
+                out=var_eps[:], in0=var_in, scalar1=scale, scalar2=EPS_LN, op0=ALU.mult, op1=ALU.add
+            )
             nc.gpsimd.tensor_tensor(out=rstd[job][:], in0=var_eps[:], in1=neg_half[:], op=ALU.pow)
 
         def centre(job):
             z[job] = z_pool.tile([P, WIDTH], F32, name="z")
-            if job in BN_JOBS:
+            if job in bn_jobs:
                 for h, cols in enumerate(halves):
                     nc.vector.scalar_tensor_tensor(
                         out=z[job][:, cols],
-                        in0=banks[(job, "sum", h)][:],
+                        in0=banks[(job, h)][:],
                         scalar=mean[job],
                         in1=gain[job[0]][:, cols],
                         op0=ALU.subtract,
@@ -328,193 +291,112 @@ def tile_rssmcell_pa_kernel(
                 )
 
         def affine(job):
-            pe_halves = PE_HALVES.get(job, ())
-            if pe_halves:
-                diag = small.tile([P, P], F32, name="diag", bufs=2)
-                nc.vector.tensor_scalar_mul(out=diag[:], in0=ident[:], scalar1=rstd[job][:])
-                for h in pe_halves:
-                    cols = halves[h]
-                    zbank[(job, h)] = turned_pool.tile([P, CHUNK], F32, name="bank")
-                    nc.tensor.matmul(out=zbank[(job, h)][:], lhsT=diag[:], rhs=z[job][:, cols], start=True, stop=False)
-                    nc.tensor.matmul(
-                        out=zbank[(job, h)][:], lhsT=ident_bf[:], rhs=bias[job[0]][:, cols], start=False, stop=True
-                    )
-            pieces = halves if job in SPLIT_JOBS or pe_halves else [slice(0, WIDTH)]
-            for h, v in enumerate(pieces):
-                if h in pe_halves:
-                    continue
-                nc.vector.scalar_tensor_tensor(
-                    out=z[job][:, v], in0=z[job][:, v], scalar=rstd[job][:], in1=bias[job[0]][:, v],
-                    op0=ALU.mult, op1=ALU.add,
-                )
-
-        def difference(m):
-            for h, cols in enumerate(halves):
-                ebank[(m, h)] = turned_pool.tile([P, CHUNK], F32, name="bank")
-                nc.tensor.matmul(
-                    out=ebank[(m, h)][:], lhsT=ident[:], rhs=value[("n", m)][:, cols], start=True, stop=False
-                )
-                nc.tensor.matmul(
-                    out=ebank[(m, h)][:], lhsT=neg_ident_bf[:], rhs=d_sb[:, m, cols], start=False, stop=True
-                )
+            nc.vector.scalar_tensor_tensor(
+                out=z[job][:], in0=z[job][:], scalar=rstd[job][:], in1=bias[job[0]][:], op0=ALU.mult, op1=ALU.add
+            )
 
         def activate(job):
             func = ACT.Tanh if job[0] == "n" else ACT.Sigmoid
-            pe_halves = PE_HALVES.get(job, ())
-            if pe_halves or job in SPLIT_JOBS:
+            nc.scalar.activation(out=value[job][:], in_=z[job][:], func=func)
+
+        def difference(job):
+            m = job[1]
+            if job[0] == "u":
+                pair = next_pair()
                 for h, cols in enumerate(halves):
-                    source_half = zbank[(job, h)][:] if h in pe_halves else z[job][:, cols]
-                    nc.scalar.activation(out=value[job][:, cols], in_=source_half, func=func)
-            else:
-                nc.scalar.activation(out=value[job][:], in_=z[job][:], func=func)
+                    bank = psum_bank(pair, h)
+                    nc.tensor.matmul(out=bank[:], lhsT=ident[:], rhs=value[("n", m)][:, cols], start=True, stop=False)
+                    nc.tensor.matmul(out=bank[:], lhsT=neg_ident_bf[:], rhs=d_sb[:, m, cols], start=False, stop=True)
+                    differences[(m, h)] = bank
 
-        def blend(job):
-            gate, m = job
-            mix = value[("n", m)]
-            if gate == "n" and m not in PESUB:
-                for cols in halves:
-                    (nc.gpsimd if GSUB else nc.vector).tensor_tensor(out=mix[:, cols], in0=mix[:, cols], in1=d_sb[:, m, cols], op=ALU.subtract)
-            if gate == "u":
+        def multiply(job):
+            m = job[1]
+            if job[0] == "u":
                 for h, cols in enumerate(halves):
-                    if m in PESUB:
-                        nc.vector.tensor_tensor(
-                            out=mix[:, cols], in0=value[job][:, cols], in1=ebank[(m, h)][:], op=ALU.mult
-                        )
-                    else:
-                        nc.vector.tensor_tensor(out=mix[:, cols], in0=mix[:, cols], in1=value[job][:, cols], op=ALU.mult)
-                for cols in halves:
-                    engine = nc.vector
-                    engine.tensor_tensor(out=mix[:, cols], in0=mix[:, cols], in1=d_sb[:, m, cols], op=ALU.add)
-                    nc.sync.dma_start(out=out[m * P : (m + 1) * P, cols], in_=mix[:, cols])
+                    nc.vector.tensor_tensor(
+                        out=value[("n", m)][:, cols], in0=value[job][:, cols], in1=differences[(m, h)][:], op=ALU.mult
+                    )
 
-        def head_pairs(i):
-            if i < 0 or head_units[i][0] not in ("ih", "hh"):
-                return []
-            which, gate, h = head_units[i]
+        gpsimd_halves = (2, 2, 1, 0)
 
-            def pair(job):
-                def run():
-                    if which == "ih":
-                        banks[(job, "sum", h)] = acc_pool.tile([P, CHUNK], F32, name="acc")
-                    passes(banks[(job, "sum", h)], head_units[i], job[1], which == "ih", which == "hh")
-
-                return run
-
-            return [pair(job) for job in jobs[:2]]
+        def finish(job):
+            m = job[1]
+            if job[0] == "u":
+                for h, cols in enumerate(halves):
+                    mix = value[("n", m)][:, cols]
+                    engine = nc.gpsimd if h >= HALVES - gpsimd_halves[m] else nc.vector
+                    engine.tensor_tensor(out=mix, in0=mix, in1=d_sb[:, m, cols], op=ALU.add)
+                    nc.sync.dma_start(out=out[m * P : (m + 1) * P, cols], in_=mix)
 
         for i in range(LOAD_AHEAD):
             load(i)
+
+        def head_sums(unit):
+            for job in jobs[:2]:
+                sums_on_unit(job, unit)
+
         for i, unit in enumerate(head_units):
-            n = blocks_of(unit)
-            pairs = head_pairs(i - 1)
-            for t in range(n):
-                turn_block(unit, t, unit[0] in ("ih", "hh") and t == n - 1)
-                if t % HWEAVE == HWEAVE - 1 and pairs:
-                    pairs.pop(0)()
-            for pair in pairs:
-                pair()
-            if i + 1 < len(head_units) and head_units[i + 1][0] == "d":
-                for m in range(ROW_TILES):
-                    mask_rows(m)
+            for t in range(BLOCKS):
+                turn_block(unit, t, unit not in (X, D) and t == BLOCKS - 1)
+            if i > 2:
+                head_sums(head_units[i - 1])
+            if unit == X:
+                mask_state()
             quantise(unit)
-            for gate in SPREAD_AT.get(i, ()):
-                gain[gate] = spread(gate, "gain")
-                bias[gate] = spread(gate, "bias")
+            if i == 2:
+                spread_to_sbuf("r")
 
         progress = {}
 
-        def due(stage, upto):
+        def advance(stage, upto):
             first = progress.get(stage, 0)
-            last = max(0, min(upto + 1, len(jobs)))
-            progress[stage] = max(first, last)
-            return jobs[first:last]
+            last = max(first, min(upto + 1, len(jobs)))
+            progress[stage] = last
+            for job in jobs[first:last]:
+                stage(job)
 
-        def job_at(index):
-            return jobs[index] if 0 <= index < len(jobs) else None
+        def turn(unit):
+            for t in range(BLOCKS):
+                turn_block(unit, t, False)
 
-        for step in range(-1, 8):
-            following = job_at(step + 1)
-            sums = gate_sums(following) if following and step > 0 else []
+        progress[sums] = 2
+        last_turn = len(later_units) - 2
+        for step in range(-1, last_turn):
+            turn(later_units[step + 1])
+            advance(centre, step - 1)
+            advance(statistics, step)
+            if step >= 0:
+                quantise(later_units[step])
+            advance(inverse_root, step)
+            advance(affine, step - 1)
+            advance(activate, step - 2)
             if step == -1:
-                sums = head_pairs(len(head_units) - 1)
-            for job in due("statistics", step):
-                statistics(job)
-            for job in due("root", step):
-                inverse_root(job)
-            for job in due("centre", step - 1):
-                centre(job)
-            for unit in step_units.get(step - 1, ()):
-                quantise(unit)
-            for unit in step_units.get(step, ()):
-                if unit[0] == "d":
-                    for m in range(unit[1], unit[1] + unit[2]):
-                        mask_rows(m)
-            for job in due("blend", step - 3):
-                blend(job)
-            for job in due("affine", step - 1):
-                affine(job)
-            turned_blocks = 0
-            for unit in step_units.get(step, ()):
-                for t in range(blocks_of(unit)):
-                    turn_block(unit, t, False)
-                    turned_blocks += 1
-                    if turned_blocks % WEAVE == 0:
-                        for pair in sums[:WEAVE]:
-                            pair()
-                        sums = sums[WEAVE:]
-            for pair in sums:
-                pair()
-            for gate, at in SPREAD_STEP.items():
-                if at == step:
-                    gain[gate] = spread(gate, "gain")
-                    bias[gate] = spread(gate, "bias")
-            for job in due("activate", step - 2):
-                activate(job)
-            for job in due("difference", step - 1):
-                if job[0] == "u" and job[1] in PESUB:
-                    difference(job[1])
-            if following:
-                gate_input(following)
-        for step in range(8, len(jobs) + 3):
-            following = job_at(step + 1)
-            sums = gate_sums(following) if following and step > 0 else []
-            if step == -1:
-                sums = head_pairs(len(head_units) - 1)
-            for job in due("statistics", step):
-                statistics(job)
-            for job in due("root", step):
-                inverse_root(job)
-            for job in due("centre", step - 1):
-                centre(job)
-            for unit in step_units.get(step - 1, ()):
-                quantise(unit)
-            for unit in step_units.get(step, ()):
-                if unit[0] == "d":
-                    for m in range(unit[1], unit[1] + unit[2]):
-                        mask_rows(m)
-            for job in due("blend", step - 3):
-                blend(job)
-            for job in due("affine", step - 1):
-                affine(job)
-            turned_blocks = 0
-            for unit in step_units.get(step, ()):
-                for t in range(blocks_of(unit)):
-                    turn_block(unit, t, False)
-                    turned_blocks += 1
-                    if turned_blocks % WEAVE == 0:
-                        for pair in sums[:WEAVE]:
-                            pair()
-                        sums = sums[WEAVE:]
-            for pair in sums:
-                pair()
-            for gate, at in SPREAD_STEP.items():
-                if at == step:
-                    gain[gate] = spread(gate, "gain")
-                    bias[gate] = spread(gate, "bias")
-            for job in due("difference", step - 1):
-                if job[0] == "u" and job[1] in PESUB:
-                    difference(job[1])
-            if following:
-                gate_input(following)
-            for job in due("activate", step - 1):
-                activate(job)
+                head_sums(head_units[-1])
+            advance(sums, step + 1)
+            if step == 1:
+                spread_to_sbuf("n")
+            advance(empty, step + 1)
+        turn(later_units[-1])
+        quantise(later_units[-2])
+        quantise(later_units[-1])
+        advance(sums, last_turn + 1)
+        advance(statistics, last_turn)
+        advance(inverse_root, last_turn)
+        advance(empty, last_turn + 1)
+        advance(centre, last_turn - 1)
+        advance(activate, last_turn - 2)
+        advance(affine, last_turn - 1)
+
+        for step in range(last_turn, len(jobs) + 2):
+            advance(sums, step + 4)
+            if step == last_turn:
+                spread_update()
+            advance(statistics, step)
+            advance(inverse_root, step)
+            advance(affine, step - 1)
+            advance(empty, step + 2)
+            advance(centre, step)
+            advance(activate, step - 2)
+            advance(difference, step - 1)
+            advance(multiply, step - 2)
+            advance(finish, step - 2)

@@ -76,8 +76,10 @@ def tile_rssmcell_pa_kernel(
 
         warm = const.tile([P, 1], F32, name="warm")
         nc.vector.memset(warm[:], 0.0)
-        ln_rows = const.tile([P, WIDTH], BF16, name="ln_rows")
-        nc.vector.memset(ln_rows[:], 0.0)
+        head_rows = const.tile([P, WIDTH], BF16, name="head_rows")
+        later_rows = const.tile([P, WIDTH], BF16, name="later_rows")
+        for rows in (head_rows, later_rows):
+            nc.vector.memset(rows[:], 0.0)
         nc.scalar.activation(out=warm[:], in_=warm[:], func=ACT.Sigmoid)
         ident = const.tile([P, P], F32, name="ident")
         make_identity(nc, ident[:])
@@ -88,18 +90,20 @@ def tile_rssmcell_pa_kernel(
         neg_ident_bf = const.tile([P, P], BF16, name="neg_ident_bf")
         nc.vector.tensor_scalar_mul(out=neg_ident_bf[:], in0=ident_bf[:], scalar1=-1.0)
         mask_sb = const.tile([P, ROW_TILES], BF16, name="mask_sb")
-        with nc.allow_non_contiguous_dma(reason="512 mask values, one to a partition for each row tile"):
-            nc.scalar.dma_start(out=mask_sb[:], in_=mask.rearrange("(m p) o -> p (m o)", p=P))
         vectors = {
-            ("r", "gain"): ln_r_g,
-            ("r", "bias"): ln_r_b,
-            ("n", "gain"): ln_n_g,
-            ("n", "bias"): ln_n_b,
-            ("u", "gain"): ln_u_g,
-            ("u", "bias"): ln_u_b,
+            ("r", "gain"): (ln_r_g, head_rows, 0),
+            ("r", "bias"): (ln_r_b, head_rows, 1),
+            ("n", "gain"): (ln_n_g, later_rows, 0),
+            ("n", "bias"): (ln_n_b, later_rows, 1),
+            ("u", "gain"): (ln_u_g, later_rows, 2),
+            ("u", "bias"): (ln_u_b, later_rows, 3),
         }
-        for row, vec in enumerate(vectors.values()):
-            nc.scalar.dma_start(out=ln_rows[row : row + 1, :], in_=vec.unsqueeze(0))
+
+        def load_vectors(gates):
+            for (gate, kind), (vec, rows, row) in vectors.items():
+                if gate in gates:
+                    nc.sync.dma_start(out=rows[row : row + 1, :], in_=vec.unsqueeze(0))
+
         d_sb = const.tile([P, ROW_TILES, K], BF16, name="d_sb")
 
         def load(i):
@@ -152,13 +156,13 @@ def tile_rssmcell_pa_kernel(
                 )
 
         def spread(bank, gate, kind):
-            row = list(vectors).index((gate, kind))
+            vec, rows, row = vectors[(gate, kind)]
             for h in range(HALVES):
                 cols = slice(h * UNIT, (h + 1) * UNIT)
                 nc.tensor.matmul(
                     out=bank[:, cols],
                     lhsT=ident_bf[:, row : row + 1].to_broadcast([P, P]),
-                    rhs=ln_rows[:, cols],
+                    rhs=rows[:, cols],
                     start=True,
                     stop=True,
                 )
@@ -317,7 +321,7 @@ def tile_rssmcell_pa_kernel(
                         out=value[("n", m)][:, cols], in0=value[job][:, cols], in1=differences[(m, h)][:], op=ALU.mult
                     )
 
-        gpsimd_halves = (2, 2, 1, 0)
+        gpsimd_halves = (1, 1, 1, 0)
 
         def finish(job):
             m = job[1]
@@ -329,6 +333,11 @@ def tile_rssmcell_pa_kernel(
                     nc.sync.dma_start(out=out[m * P : (m + 1) * P, cols], in_=mix)
 
         for i in range(LOAD_AHEAD):
+            if i == BLOCKS:
+                with nc.allow_non_contiguous_dma(reason="512 mask values, one to a partition for each row tile"):
+                    nc.sync.dma_start(out=mask_sb[:], in_=mask.rearrange("(m p) o -> p (m o)", p=P))
+            if i == 2 * BLOCKS:
+                load_vectors("r")
             load(i)
 
         def head_sums(unit):
@@ -345,6 +354,7 @@ def tile_rssmcell_pa_kernel(
             quantise(unit)
             if i == 2:
                 spread_to_sbuf("r")
+        load_vectors("nu")
 
         progress = {}
 

@@ -76,10 +76,10 @@ def tile_rssmcell_pa_kernel(
 
         warm = const.tile([P, 1], F32, name="warm")
         nc.vector.memset(warm[:], 0.0)
-        head_rows = const.tile([P, WIDTH], BF16, name="head_rows")
-        later_rows = const.tile([P, WIDTH], BF16, name="later_rows")
-        for rows in (head_rows, later_rows):
-            nc.vector.memset(rows[:], 0.0)
+        vector_rows = {}
+        for gate in ("r", "u"):
+            vector_rows[gate] = const.tile([P, WIDTH], BF16, name="rows_" + gate)
+            nc.vector.memset(vector_rows[gate][:], 0.0)
         nc.scalar.activation(out=warm[:], in_=warm[:], func=ACT.Sigmoid)
         ident = const.tile([P, P], F32, name="ident")
         make_identity(nc, ident[:])
@@ -89,24 +89,38 @@ def tile_rssmcell_pa_kernel(
         nc.gpsimd.memset(neg_half[:], -0.5)
         neg_ident_bf = const.tile([P, P], BF16, name="neg_ident_bf")
         nc.vector.tensor_scalar_mul(out=neg_ident_bf[:], in0=ident_bf[:], scalar1=-1.0)
+        eps = const.tile([P, 1], F32, name="eps")
+        nc.vector.tensor_scalar(
+            out=eps[:], in0=ident[:, 0:1], scalar1=0.0, scalar2=EPS_LN, op0=ALU.mult, op1=ALU.add
+        )
         mask_sb = const.tile([P, ROW_TILES], BF16, name="mask_sb")
         vectors = {
-            ("r", "gain"): (ln_r_g, head_rows, 0),
-            ("r", "bias"): (ln_r_b, head_rows, 1),
-            ("n", "gain"): (ln_n_g, later_rows, 0),
-            ("n", "bias"): (ln_n_b, later_rows, 1),
-            ("u", "gain"): (ln_u_g, later_rows, 2),
-            ("u", "bias"): (ln_u_b, later_rows, 3),
+            ("r", "gain"): ln_r_g,
+            ("r", "bias"): ln_r_b,
+            ("n", "gain"): ln_n_g,
+            ("n", "bias"): ln_n_b,
+            ("u", "gain"): ln_u_g,
+            ("u", "bias"): ln_u_b,
         }
+        kinds = ("gain", "bias")
+        gain = {}
+        bias = {}
 
-        def load_vectors(gates):
-            for (gate, kind), (vec, rows, row) in vectors.items():
-                if gate in gates:
-                    nc.sync.dma_start(out=rows[row : row + 1, :], in_=vec.unsqueeze(0))
+        def load_rows(gate):
+            for row, kind in enumerate(kinds):
+                vec = vectors[(gate, kind)]
+                nc.sync.dma_start(out=vector_rows[gate][row : row + 1, :], in_=vec.unsqueeze(0))
+
+        def broadcast_newval():
+            for kind, kept in zip(kinds, (gain, bias)):
+                kept["n"] = const.tile([P, WIDTH], BF16, name=kind + "_n")
+                nc.sync.dma_start(out=kept["n"][:], in_=vectors[("n", kind)].partition_broadcast(P))
 
         d_sb = const.tile([P, ROW_TILES, K], BF16, name="d_sb")
 
         def load(i):
+            if i == len(stream) - 10:
+                broadcast_newval()
             if i < len(stream):
                 unit, t = stream[i]
                 row = t * P
@@ -155,35 +169,32 @@ def tile_rssmcell_pa_kernel(
                     stop=(last and g == PASSES - 1),
                 )
 
-        def spread(bank, gate, kind):
-            vec, rows, row = vectors[(gate, kind)]
+        def spread(bank, gate, row):
             for h in range(HALVES):
                 cols = slice(h * UNIT, (h + 1) * UNIT)
                 nc.tensor.matmul(
                     out=bank[:, cols],
                     lhsT=ident_bf[:, row : row + 1].to_broadcast([P, P]),
-                    rhs=rows[:, cols],
+                    rhs=vector_rows[gate][:, cols],
                     start=True,
                     stop=True,
                 )
 
-        gain = {}
-        bias = {}
-
-        def spread_to_sbuf(gate):
-            for kind, kept in (("gain", gain), ("bias", bias)):
+        def spread_reset():
+            for row, kept in enumerate((gain, bias)):
                 bank = turned_bank((P, WIDTH), BF16)
-                spread(bank, gate, kind)
-                kept[gate] = const.tile([P, WIDTH], BF16, name=kind + "_" + gate)
-                nc.scalar.copy(out=kept[gate][:], in_=bank[:])
+                spread(bank, "r", row)
+                kept["r"] = const.tile([P, WIDTH], BF16, name=kinds[row] + "_r")
+                nc.scalar.copy(out=kept["r"][:], in_=bank[:])
 
         def spread_update():
-            for i, (kind, kept) in enumerate((("gain", gain), ("bias", bias))):
-                kept["u"] = psum_bank(1, i, (P, WIDTH), BF16)
-                spread(kept["u"], "u", kind)
+            for row, kept in enumerate((gain, bias)):
+                kept["u"] = psum_bank(1, row, (P, WIDTH), BF16)
+                spread(kept["u"], "u", row)
 
         jobs = [(gate, m) for gate in ("r", "n", "u") for m in range(ROW_TILES)]
         bn_jobs = (("r", 0), ("r", 2))
+        vector_half = {("r", 1): 0, ("u", 1): 1, ("u", 3): 1}
         value = {}
         half_sums = {}
         mean = {}
@@ -234,12 +245,36 @@ def tile_rssmcell_pa_kernel(
                     )
             elif job not in bn_jobs:
                 for h, cols in enumerate(halves):
-                    nc.scalar.activation(
-                        out=value[job][:, cols],
-                        in_=banks[(job, h)][:],
-                        func=ACT.Identity,
-                        accum_out=half_sums[job][:, h : h + 1],
-                    )
+                    if vector_half.get(job) == h:
+                        nc.vector.tensor_scalar(
+                            out=value[job][:, cols],
+                            in0=banks[(job, h)][:],
+                            scalar1=1.0,
+                            scalar2=0.0,
+                            op0=ALU.mult,
+                            op1=ALU.add,
+                            accum_out=half_sums[job][:, h : h + 1],
+                        )
+                    else:
+                        nc.scalar.activation(
+                            out=value[job][:, cols],
+                            in_=banks[(job, h)][:],
+                            func=ACT.Identity,
+                            accum_out=half_sums[job][:, h : h + 1],
+                        )
+
+        def mean_of(job):
+            if job not in bn_jobs:
+                scaled_sums = small.tile([P, HALVES], F32, name="scaled_sums")
+                neg_mean = small.tile([P, 1], F32, name="neg_mean")
+                nc.scalar.activation(
+                    out=scaled_sums[:],
+                    in_=half_sums[job][:],
+                    func=ACT.Identity,
+                    scale=-1.0 / WIDTH,
+                    accum_out=neg_mean[:],
+                )
+                mean[job] = neg_mean[:]
 
         def statistics(job):
             if job in bn_jobs:
@@ -251,20 +286,10 @@ def tile_rssmcell_pa_kernel(
                 mean[job] = moments[:, 0:1]
                 variance[job] = (moments[:, 1:2], 1.0)
             else:
-                scaled_sums = small.tile([P, HALVES], F32, name="scaled_sums")
-                neg_mean = small.tile([P, 1], F32, name="neg_mean")
-                nc.scalar.activation(
-                    out=scaled_sums[:],
-                    in_=half_sums[job][:],
-                    func=ACT.Identity,
-                    scale=-1.0 / WIDTH,
-                    accum_out=neg_mean[:],
-                )
-                mean[job] = neg_mean[:]
                 squares = squares_pool.tile([P, WIDTH], BF16, name="squares")
                 sum_sq = small.tile([P, 1], F32, name="sum_sq")
                 nc.scalar.activation(
-                    out=squares[:], in_=value[job][:], func=ACT.Square, bias=neg_mean[:], accum_out=sum_sq[:]
+                    out=squares[:], in_=value[job][:], func=ACT.Square, bias=mean[job], accum_out=sum_sq[:]
                 )
                 variance[job] = (sum_sq[:], 1.0 / WIDTH)
 
@@ -272,9 +297,7 @@ def tile_rssmcell_pa_kernel(
             var_eps = small.tile([P, 1], F32, name="var_eps")
             rstd[job] = small.tile([P, 1], F32, name="rstd")
             var_in, scale = variance[job]
-            nc.gpsimd.tensor_scalar(
-                out=var_eps[:], in0=var_in, scalar1=scale, scalar2=EPS_LN, op0=ALU.mult, op1=ALU.add
-            )
+            nc.scalar.activation(out=var_eps[:], in_=var_in, func=ACT.Identity, scale=scale, bias=eps[:])
             nc.gpsimd.tensor_tensor(out=rstd[job][:], in0=var_eps[:], in1=neg_half[:], op=ALU.pow)
 
         def centre(job):
@@ -321,7 +344,7 @@ def tile_rssmcell_pa_kernel(
                         out=value[("n", m)][:, cols], in0=value[job][:, cols], in1=differences[(m, h)][:], op=ALU.mult
                     )
 
-        gpsimd_halves = (1, 1, 1, 0)
+        gpsimd_halves = (2, 1, 0, 0)
 
         def finish(job):
             m = job[1]
@@ -337,7 +360,7 @@ def tile_rssmcell_pa_kernel(
                 with nc.allow_non_contiguous_dma(reason="512 mask values, one to a partition for each row tile"):
                     nc.sync.dma_start(out=mask_sb[:], in_=mask.rearrange("(m p) o -> p (m o)", p=P))
             if i == 2 * BLOCKS:
-                load_vectors("r")
+                load_rows("r")
             load(i)
 
         def head_sums(unit):
@@ -353,8 +376,8 @@ def tile_rssmcell_pa_kernel(
                 mask_state()
             quantise(unit)
             if i == 2:
-                spread_to_sbuf("r")
-        load_vectors("nu")
+                spread_reset()
+        load_rows("u")
 
         progress = {}
 
@@ -374,39 +397,40 @@ def tile_rssmcell_pa_kernel(
         for step in range(-1, last_turn):
             turn(later_units[step + 1])
             advance(centre, step - 1)
+            advance(mean_of, step)
             advance(statistics, step)
             if step >= 0:
                 quantise(later_units[step])
             advance(inverse_root, step)
-            advance(affine, step - 1)
-            advance(activate, step - 2)
             if step == -1:
                 head_sums(head_units[-1])
             advance(sums, step + 1)
-            if step == 1:
-                spread_to_sbuf("n")
+            advance(affine, step - 1)
+            advance(activate, step - 2)
             advance(empty, step + 1)
         turn(later_units[-1])
         quantise(later_units[-2])
-        quantise(later_units[-1])
-        advance(sums, last_turn + 1)
+        advance(mean_of, last_turn)
         advance(statistics, last_turn)
         advance(inverse_root, last_turn)
-        advance(empty, last_turn + 1)
         advance(centre, last_turn - 1)
+        quantise(later_units[-1])
+        advance(sums, last_turn + 1)
         advance(activate, last_turn - 2)
+        advance(empty, last_turn + 1)
         advance(affine, last_turn - 1)
 
-        for step in range(last_turn, len(jobs) + 2):
-            advance(sums, step + 4)
-            if step == last_turn:
-                spread_update()
+        for step in range(last_turn, len(jobs) + 3):
+            advance(finish, step - 3)
+            advance(sums, step + 3)
+            advance(mean_of, step)
             advance(statistics, step)
-            advance(inverse_root, step)
-            advance(affine, step - 1)
-            advance(empty, step + 2)
-            advance(centre, step)
+            if step == last_turn + 1:
+                spread_update()
+            advance(difference, step)
             advance(activate, step - 2)
-            advance(difference, step - 1)
+            advance(centre, step)
+            advance(affine, step - 1)
             advance(multiply, step - 2)
-            advance(finish, step - 2)
+            advance(empty, step + 3)
+            advance(inverse_root, step)

@@ -119,7 +119,7 @@ def tile_rssmcell_pa_kernel(
         d_sb = const.tile([P, ROW_TILES, K], BF16, name="d_sb")
 
         def load(i):
-            if i == len(stream) - 10:
+            if i == len(stream) - 8:
                 broadcast_newval()
             if i < len(stream):
                 unit, t = stream[i]
@@ -194,7 +194,8 @@ def tile_rssmcell_pa_kernel(
 
         jobs = [(gate, m) for gate in ("r", "n", "u") for m in range(ROW_TILES)]
         bn_jobs = (("r", 0), ("r", 2))
-        vector_half = {("r", 1): 0, ("u", 1): 1, ("u", 3): 1}
+        vector_empties = ("u", 2)
+        tensor_affine = ("n", 1)
         value = {}
         half_sums = {}
         mean = {}
@@ -202,6 +203,7 @@ def tile_rssmcell_pa_kernel(
         rstd = {}
         z = {}
         banks = {}
+        affine_banks = []
         differences = {}
         halves = [slice(h * UNIT, (h + 1) * UNIT) for h in range(HALVES)]
         for job in jobs:
@@ -221,9 +223,12 @@ def tile_rssmcell_pa_kernel(
                     banks[(job, h)] = psum_bank(pairs[job], h)
                 passes(banks[(job, h)], unit, m, which == "ih", which == "hh")
 
+        def in_head(job, unit):
+            return job == jobs[0] or (job == jobs[1] and unit[2] == 0)
+
         def sums(job):
             for unit in units:
-                if unit not in (X, D) and unit[1] == job[0]:
+                if unit not in (X, D) and unit[1] == job[0] and not in_head(job, unit):
                     sums_on_unit(job, unit)
 
         def empty(job):
@@ -245,7 +250,7 @@ def tile_rssmcell_pa_kernel(
                     )
             elif job not in bn_jobs:
                 for h, cols in enumerate(halves):
-                    if vector_half.get(job) == h:
+                    if job == vector_empties:
                         nc.vector.tensor_scalar(
                             out=value[job][:, cols],
                             in0=banks[(job, h)][:],
@@ -318,13 +323,28 @@ def tile_rssmcell_pa_kernel(
                 )
 
         def affine(job):
+            if job == tensor_affine:
+                diag = small.tile([P, P], F32, name="diag", bufs=1)
+                nc.gpsimd.tensor_scalar(
+                    out=diag[:], in0=ident[:], scalar1=rstd[job][:], scalar2=0.0, op0=ALU.mult, op1=ALU.add
+                )
+                for h, cols in enumerate(halves):
+                    bank = psum_bank(1, h)
+                    nc.tensor.matmul(out=bank[:], lhsT=diag[:], rhs=z[job][:, cols], start=True, stop=False)
+                    nc.tensor.matmul(out=bank[:], lhsT=ident_bf[:], rhs=bias[job[0]][:, cols], start=False, stop=True)
+                    affine_banks.append(bank)
+                return
             nc.vector.scalar_tensor_tensor(
                 out=z[job][:], in0=z[job][:], scalar=rstd[job][:], in1=bias[job[0]][:], op0=ALU.mult, op1=ALU.add
             )
 
         def activate(job):
             func = ACT.Tanh if job[0] == "n" else ACT.Sigmoid
-            nc.scalar.activation(out=value[job][:], in_=z[job][:], func=func)
+            if job == tensor_affine:
+                for cols, bank in zip(halves, affine_banks):
+                    nc.scalar.activation(out=value[job][:, cols], in_=bank[:], func=func)
+            else:
+                nc.scalar.activation(out=value[job][:], in_=z[job][:], func=func)
 
         def difference(job):
             m = job[1]
@@ -344,7 +364,7 @@ def tile_rssmcell_pa_kernel(
                         out=value[("n", m)][:, cols], in0=value[job][:, cols], in1=differences[(m, h)][:], op=ALU.mult
                     )
 
-        gpsimd_halves = (2, 1, 0, 0)
+        gpsimd_halves = (1, 1, 1, 0)
 
         def finish(job):
             m = job[1]
@@ -365,7 +385,8 @@ def tile_rssmcell_pa_kernel(
 
         def head_sums(unit):
             for job in jobs[:2]:
-                sums_on_unit(job, unit)
+                if in_head(job, unit):
+                    sums_on_unit(job, unit)
 
         for i, unit in enumerate(head_units):
             for t in range(BLOCKS):
@@ -392,12 +413,11 @@ def tile_rssmcell_pa_kernel(
             for t in range(BLOCKS):
                 turn_block(unit, t, False)
 
-        progress[sums] = 2
         last_turn = len(later_units) - 2
         for step in range(-1, last_turn):
+            advance(mean_of, step)
             turn(later_units[step + 1])
             advance(centre, step - 1)
-            advance(mean_of, step)
             advance(statistics, step)
             if step >= 0:
                 quantise(later_units[step])
@@ -406,31 +426,31 @@ def tile_rssmcell_pa_kernel(
                 head_sums(head_units[-1])
             advance(sums, step + 1)
             advance(affine, step - 1)
-            advance(activate, step - 2)
             advance(empty, step + 1)
-        turn(later_units[-1])
-        quantise(later_units[-2])
+            advance(activate, step - 2)
         advance(mean_of, last_turn)
-        advance(statistics, last_turn)
-        advance(inverse_root, last_turn)
+        turn(later_units[-1])
         advance(centre, last_turn - 1)
-        quantise(later_units[-1])
+        quantise(later_units[-2])
         advance(sums, last_turn + 1)
-        advance(activate, last_turn - 2)
-        advance(empty, last_turn + 1)
+        advance(statistics, last_turn)
         advance(affine, last_turn - 1)
+        advance(inverse_root, last_turn)
+        advance(empty, last_turn + 1)
+        advance(activate, last_turn - 2)
+        quantise(later_units[-1])
 
-        for step in range(last_turn, len(jobs) + 3):
-            advance(finish, step - 3)
-            advance(sums, step + 3)
-            advance(mean_of, step)
-            advance(statistics, step)
-            if step == last_turn + 1:
+        for step in range(last_turn, len(jobs) + 2):
+            advance(empty, step + 1)
+            advance(sums, step + 2)
+            if step == last_turn:
                 spread_update()
             advance(difference, step)
-            advance(activate, step - 2)
+            advance(mean_of, step + 1)
+            advance(statistics, step)
+            advance(inverse_root, step)
             advance(centre, step)
             advance(affine, step - 1)
             advance(multiply, step - 2)
-            advance(empty, step + 3)
-            advance(inverse_root, step)
+            advance(finish, step - 2)
+            advance(activate, step - 1)

from contextlib import ExitStack

import concourse.mybir as mybir
from concourse.masks import make_identity

F32 = mybir.dt.float32
BF16 = mybir.dt.bfloat16
U32 = mybir.dt.uint32
U8 = mybir.dt.uint8
FP8X4 = mybir.dt.float8_e4m3fn_x4
ALU = mybir.AluOpType
ACT = mybir.ActivationFunctionType

P = 128
BATCH = 512
K = 1024
WIDTH = 1024
UNIT = 512
BLOCKS = UNIT // P
PASSES = K // 512
ROW_TILES = BATCH // P
HALVES = WIDTH // UNIT
EPS_LN = 1e-3
RAW_BLOCKS = 16
LOAD_AHEAD = 12

FLOPS = 2 * 2 * BATCH * K * 3 * WIDTH


def tile_rssmcell_pa_kernel(
    tc, x_pre, deter, mask, w_ih, w_hh, ln_r_g, ln_r_b, ln_u_g, ln_u_b, ln_n_g, ln_n_b, out
):
    nc = tc.nc
    with ExitStack() as ctx:
        const = ctx.enter_context(tc.tile_pool(name="const", bufs=1))
        raw_pool = ctx.enter_context(tc.tile_pool(name="raw", bufs=RAW_BLOCKS))
        grouped_pool = ctx.enter_context(tc.tile_pool(name="grouped", bufs=3))
        gate_pool = ctx.enter_context(tc.tile_pool(name="gate", bufs=ROW_TILES))
        z_pool = ctx.enter_context(tc.tile_pool(name="z", bufs=3))
        squares_pool = ctx.enter_context(tc.tile_pool(name="squares", bufs=2))
        small = ctx.enter_context(tc.tile_pool(name="small", bufs=8))
        psum = ctx.enter_context(tc.psum_pool(name="psum", bufs=1))
        ctx.enter_context(tc.manual_schedule())

        source = {"x": x_pre, "d": deter, "ih": w_ih, "hh": w_hh}
        gate_rows = {"r": 0, "u": WIDTH, "n": 2 * WIDTH}
        X, D = ("x",), ("d",)
        head_units = [X, D] + [(which, "r", h) for h in range(HALVES) for which in ("ih", "hh")]
        later_units = [(which, "n", h) for h in range(HALVES) for which in ("hh", "ih")]
        later_units += [(which, "u", h) for h in range(HALVES) for which in ("ih", "hh")]
        units = head_units + later_units
        codes = {}
        scales = {}
        for i, unit in enumerate(units):
            codes[unit] = const.tile([P, PASSES * UNIT], U32, align_bytes=64, name="codes%d" % i)
            scales[unit] = const.tile([P, PASSES * UNIT], U8, align_bytes=64, name="scales%d" % i)
        stream = [(unit, t) for unit in units for t in range(BLOCKS)]
        raw = {}
        grouped = {}

        def psum_bank(pair, i, shape=(P, UNIT), dtype=F32):
            return psum.tile(list(shape), dtype, name="bank%d" % (2 * pair + i))

        turned = []

        def turned_bank(shape=(P, UNIT), dtype=F32):
            turned.append(len(turned) % 4)
            return psum_bank(turned[-1] // 2, turned[-1] % 2, shape, dtype)

        taken = []
        pairs = {}

        def next_pair():
            taken.append((0, 2, 3)[len(taken) % 3])
            return taken[-1]

        warm = const.tile([P, 1], F32, name="warm")
        nc.vector.memset(warm[:], 0.0)
        vector_rows = {}
        for gate in ("r", "u"):
            vector_rows[gate] = const.tile([P, WIDTH], BF16, name="rows_" + gate)
            nc.vector.memset(vector_rows[gate][:], 0.0)
        nc.scalar.activation(out=warm[:], in_=warm[:], func=ACT.Sigmoid)
        ident = const.tile([P, P], F32, name="ident")
        make_identity(nc, ident[:])
        ident_bf = const.tile([P, P], BF16, name="ident_bf")
        make_identity(nc, ident_bf[:])
        neg_half = const.tile([P, 1], F32, name="neg_half")
        nc.gpsimd.memset(neg_half[:], -0.5)
        neg_ident_bf = const.tile([P, P], BF16, name="neg_ident_bf")
        nc.vector.tensor_scalar_mul(out=neg_ident_bf[:], in0=ident_bf[:], scalar1=-1.0)
        eps = const.tile([P, 1], F32, name="eps")
        nc.vector.tensor_scalar(
            out=eps[:], in0=ident[:, 0:1], scalar1=0.0, scalar2=EPS_LN, op0=ALU.mult, op1=ALU.add
        )
        mask_sb = const.tile([P, ROW_TILES], BF16, name="mask_sb")
        vectors = {
            ("r", "gain"): ln_r_g,
            ("r", "bias"): ln_r_b,
            ("n", "gain"): ln_n_g,
            ("n", "bias"): ln_n_b,
            ("u", "gain"): ln_u_g,
            ("u", "bias"): ln_u_b,
        }
        kinds = ("gain", "bias")
        gain = {}
        bias = {}

        def load_rows(gate):
            for row, kind in enumerate(kinds):
                vec = vectors[(gate, kind)]
                nc.sync.dma_start(out=vector_rows[gate][row : row + 1, :], in_=vec.unsqueeze(0))

        def broadcast_newval():
            for kind, kept in zip(kinds, (gain, bias)):
                kept["n"] = const.tile([P, WIDTH], BF16, name=kind + "_n")
                nc.sync.dma_start(out=kept["n"][:], in_=vectors[("n", kind)].partition_broadcast(P))

        d_sb = const.tile([P, ROW_TILES, K], BF16, name="d_sb")

        def load(i):
            if i == len(stream) - 8:
                broadcast_newval()
            if i < len(stream):
                unit, t = stream[i]
                row = t * P
                if unit not in (X, D):
                    row += gate_rows[unit[1]] + unit[2] * UNIT
                raw[(unit, t)] = raw_pool.tile([P, K], BF16, name="raw")
                nc.sync.dma_start(out=raw[(unit, t)][:], in_=source[unit[0]][row : row + P, :])

        def mask_state():
            for m in range(ROW_TILES):
                nc.vector.tensor_scalar_mul(out=d_sb[:, m, :], in0=raw[(D, m)][:], scalar1=mask_sb[:, m : m + 1])

        def turn_block(unit, t, on_vector):
            if t == 0:
                grouped[unit] = grouped_pool.tile([P, 4 * PASSES * UNIT], BF16, align_bytes=64, name="grouped")
            load(stream.index((unit, t)) + LOAD_AHEAD)
            words = (d_sb[:, t, :] if unit == D else raw[(unit, t)][:]).bitcast(F32)
            bank = turned_bank()
            for a in range(2 * PASSES):
                nc.tensor.transpose(
                    out=bank[:, a * P : (a + 1) * P], in_=words[:, a * P : (a + 1) * P], identity=ident[:]
                )
            grouped_words = grouped[unit][:].bitcast(F32).rearrange("p (g c u) -> p g c u", g=PASSES, u=2)
            into = grouped_words[:, :, t * P : (t + 1) * P, :]
            words_out = bank[:].rearrange("p (g u c) -> p g c u", g=PASSES, u=2)
            if on_vector:
                nc.vector.tensor_copy(out=into, in_=words_out)
            else:
                nc.scalar.copy(out=into, in_=words_out)

        def quantise(unit):
            nc.vector.quantize_mx(out=codes[unit][:].bitcast(FP8X4), scales=scales[unit][:], in_=grouped[unit][:])

        def passes(bank, unit, m, first, last):
            act = X if unit[0] == "ih" else D
            for g in range(PASSES):
                rows = slice(g * UNIT + m * P, g * UNIT + (m + 1) * P)
                cols = slice(g * UNIT, (g + 1) * UNIT)
                nc.tensor.matmul_mx(
                    out=bank[:],
                    lhsT=codes[act][:, rows].bitcast(FP8X4),
                    lhsT_scale=scales[act][:, rows],
                    rhs=codes[unit][:, cols].bitcast(FP8X4),
                    rhs_scale=scales[unit][:, cols],
                    start=(first and g == 0),
                    stop=(last and g == PASSES - 1),
                )

        def spread(bank, gate, row):
            for h in range(HALVES):
                cols = slice(h * UNIT, (h + 1) * UNIT)
                nc.tensor.matmul(
                    out=bank[:, cols],
                    lhsT=ident_bf[:, row : row + 1].to_broadcast([P, P]),
                    rhs=vector_rows[gate][:, cols],
                    start=True,
                    stop=True,
                )

        def spread_reset():
            for row, kept in enumerate((gain, bias)):
                bank = turned_bank((P, WIDTH), BF16)
                spread(bank, "r", row)
                kept["r"] = const.tile([P, WIDTH], BF16, name=kinds[row] + "_r")
                nc.scalar.copy(out=kept["r"][:], in_=bank[:])

        def spread_update():
            for row, kept in enumerate((gain, bias)):
                kept["u"] = psum_bank(1, row, (P, WIDTH), BF16)
                spread(kept["u"], "u", row)

        jobs = [(gate, m) for gate in ("r", "n", "u") for m in range(ROW_TILES)]
        bn_jobs = (("r", 0), ("r", 2))
        vector_empties = ("u", 2)
        tensor_affine = ("n", 1)
        value = {}
        half_sums = {}
        mean = {}
        variance = {}
        rstd = {}
        z = {}
        banks = {}
        affine_banks = []
        differences = {}
        halves = [slice(h * UNIT, (h + 1) * UNIT) for h in range(HALVES)]
        for job in jobs:
            value[job] = gate_pool.tile([P, WIDTH], F32, name=job[0] + "_gate")
            half_sums[job] = small.tile([P, HALVES], F32, name="half_sums", bufs=len(jobs))

        def sums_on_unit(job, unit):
            which, gate, h = unit
            m = job[1]
            if gate == "n":
                banks[(job, which, h)] = psum_bank(2 + h, 0 if which == "hh" else 1)
                passes(banks[(job, which, h)], unit, m, True, True)
            else:
                if which == "ih":
                    if h == 0:
                        pairs[job] = 2 + m % 2 if gate == "r" else next_pair()
                    banks[(job, h)] = psum_bank(pairs[job], h)
                passes(banks[(job, h)], unit, m, which == "ih", which == "hh")

        def in_head(job, unit):
            return job == jobs[0] or (job == jobs[1] and unit[2] == 0)

        def sums(job):
            for unit in units:
                if unit not in (X, D) and unit[1] == job[0] and not in_head(job, unit):
                    sums_on_unit(job, unit)

        def empty(job):
            gate, m = job
            if gate == "n":
                for h, cols in enumerate(halves):
                    nc.vector.tensor_tensor(
                        out=value[job][:, cols], in0=value[("r", m)][:, cols], in1=banks[(job, "hh", h)][:], op=ALU.mult
                    )
                for h, cols in enumerate(halves):
                    nc.vector.scalar_tensor_tensor(
                        out=value[job][:, cols],
                        in0=value[job][:, cols],
                        scalar=1.0,
                        in1=banks[(job, "ih", h)][:],
                        op0=ALU.mult,
                        op1=ALU.add,
                        accum_out=half_sums[job][:, h : h + 1],
                    )
            elif job not in bn_jobs:
                for h, cols in enumerate(halves):
                    if job == vector_empties:
                        nc.vector.tensor_scalar(
                            out=value[job][:, cols],
                            in0=banks[(job, h)][:],
                            scalar1=1.0,
                            scalar2=0.0,
                            op0=ALU.mult,
                            op1=ALU.add,
                            accum_out=half_sums[job][:, h : h + 1],
                        )
                    else:
                        nc.scalar.activation(
                            out=value[job][:, cols],
                            in_=banks[(job, h)][:],
                            func=ACT.Identity,
                            accum_out=half_sums[job][:, h : h + 1],
                        )

        def mean_of(job):
            if job not in bn_jobs:
                scaled_sums = small.tile([P, HALVES], F32, name="scaled_sums")
                neg_mean = small.tile([P, 1], F32, name="neg_mean")
                nc.scalar.activation(
                    out=scaled_sums[:],
                    in_=half_sums[job][:],
                    func=ACT.Identity,
                    scale=-1.0 / WIDTH,
                    accum_out=neg_mean[:],
                )
                mean[job] = neg_mean[:]

        def statistics(job):
            if job in bn_jobs:
                pieces = small.tile([P, HALVES, 6], F32, name="pieces")
                for h in range(HALVES):
                    nc.vector.bn_stats(out=pieces[:, h, :], in_=banks[(job, h)][:])
                moments = small.tile([P, 2], F32, name="moments")
                nc.vector.bn_aggr(out=moments[:], in_=pieces[:].rearrange("p h s -> p (h s)"))
                mean[job] = moments[:, 0:1]
                variance[job] = (moments[:, 1:2], 1.0)
            else:
                squares = squares_pool.tile([P, WIDTH], BF16, name="squares")
                sum_sq = small.tile([P, 1], F32, name="sum_sq")
                nc.scalar.activation(
                    out=squares[:], in_=value[job][:], func=ACT.Square, bias=mean[job], accum_out=sum_sq[:]
                )
                variance[job] = (sum_sq[:], 1.0 / WIDTH)

        def inverse_root(job):
            var_eps = small.tile([P, 1], F32, name="var_eps")
            rstd[job] = small.tile([P, 1], F32, name="rstd")
            var_in, scale = variance[job]
            nc.scalar.activation(out=var_eps[:], in_=var_in, func=ACT.Identity, scale=scale, bias=eps[:])
            nc.gpsimd.tensor_tensor(out=rstd[job][:], in0=var_eps[:], in1=neg_half[:], op=ALU.pow)

        def centre(job):
            z[job] = z_pool.tile([P, WIDTH], F32, name="z")
            if job in bn_jobs:
                for h, cols in enumerate(halves):
                    nc.vector.scalar_tensor_tensor(
                        out=z[job][:, cols],
                        in0=banks[(job, h)][:],
                        scalar=mean[job],
                        in1=gain[job[0]][:, cols],
                        op0=ALU.subtract,
                        op1=ALU.mult,
                    )
            else:
                nc.vector.scalar_tensor_tensor(
                    out=z[job][:], in0=value[job][:], scalar=mean[job], in1=gain[job[0]][:], op0=ALU.add, op1=ALU.mult
                )

        def affine(job):
            if job == tensor_affine:
                diag = small.tile([P, P], F32, name="diag", bufs=1)
                nc.gpsimd.tensor_scalar(
                    out=diag[:], in0=ident[:], scalar1=rstd[job][:], scalar2=0.0, op0=ALU.mult, op1=ALU.add
                )
                for h, cols in enumerate(halves):
                    bank = psum_bank(1, h)
                    nc.tensor.matmul(out=bank[:], lhsT=diag[:], rhs=z[job][:, cols], start=True, stop=False)
                    nc.tensor.matmul(out=bank[:], lhsT=ident_bf[:], rhs=bias[job[0]][:, cols], start=False, stop=True)
                    affine_banks.append(bank)
                return
            nc.vector.scalar_tensor_tensor(
                out=z[job][:], in0=z[job][:], scalar=rstd[job][:], in1=bias[job[0]][:], op0=ALU.mult, op1=ALU.add
            )

        def activate(job):
            func = ACT.Tanh if job[0] == "n" else ACT.Sigmoid
            if job == tensor_affine:
                for cols, bank in zip(halves, affine_banks):
                    nc.scalar.activation(out=value[job][:, cols], in_=bank[:], func=func)
            else:
                nc.scalar.activation(out=value[job][:], in_=z[job][:], func=func)

        def difference(job):
            m = job[1]
            if job[0] == "u":
                pair = next_pair()
                for h, cols in enumerate(halves):
                    bank = psum_bank(pair, h)
                    nc.tensor.matmul(out=bank[:], lhsT=ident[:], rhs=value[("n", m)][:, cols], start=True, stop=False)
                    nc.tensor.matmul(out=bank[:], lhsT=neg_ident_bf[:], rhs=d_sb[:, m, cols], start=False, stop=True)
                    differences[(m, h)] = bank

        def multiply(job):
            m = job[1]
            if job[0] == "u":
                for h, cols in enumerate(halves):
                    nc.vector.tensor_tensor(
                        out=value[("n", m)][:, cols], in0=value[job][:, cols], in1=differences[(m, h)][:], op=ALU.mult
                    )

        gpsimd_halves = (1, 1, 1, 0)

        def finish(job):
            m = job[1]
            if job[0] == "u":
                for h, cols in enumerate(halves):
                    mix = value[("n", m)][:, cols]
                    engine = nc.gpsimd if h >= HALVES - gpsimd_halves[m] else nc.vector
                    engine.tensor_tensor(out=mix, in0=mix, in1=d_sb[:, m, cols], op=ALU.add)
                    nc.sync.dma_start(out=out[m * P : (m + 1) * P, cols], in_=mix)

        for i in range(LOAD_AHEAD):
            if i == BLOCKS:
                with nc.allow_non_contiguous_dma(reason="512 mask values, one to a partition for each row tile"):
                    nc.sync.dma_start(out=mask_sb[:], in_=mask.rearrange("(m p) o -> p (m o)", p=P))
            if i == 2 * BLOCKS:
                load_rows("r")
            load(i)

        def head_sums(unit):
            for job in jobs[:2]:
                if in_head(job, unit):
                    sums_on_unit(job, unit)

        for i, unit in enumerate(head_units):
            for t in range(BLOCKS):
                turn_block(unit, t, unit not in (X, D) and t == BLOCKS - 1)
            if i > 2:
                head_sums(head_units[i - 1])
            if unit == X:
                mask_state()
            quantise(unit)
            if i == 2:
                spread_reset()
        load_rows("u")

        progress = {}

        def advance(stage, upto):
            first = progress.get(stage, 0)
            last = max(first, min(upto + 1, len(jobs)))
            progress[stage] = last
            for job in jobs[first:last]:
                stage(job)

        def turn(unit):
            for t in range(BLOCKS):
                turn_block(unit, t, False)

        last_turn = len(later_units) - 2
        for step in range(-1, last_turn):
            advance(mean_of, step)
            turn(later_units[step + 1])
            advance(centre, step - 1)
            advance(statistics, step)
            if step >= 0:
                quantise(later_units[step])
            advance(inverse_root, step)
            if step == -1:
                head_sums(head_units[-1])
            advance(sums, step + 1)
            advance(affine, step - 1)
            advance(empty, step + 1)
            advance(activate, step - 2)
        advance(mean_of, last_turn)
        turn(later_units[-1])
        advance(centre, last_turn - 1)
        quantise(later_units[-2])
        advance(sums, last_turn + 1)
        advance(statistics, last_turn)
        advance(affine, last_turn - 1)
        advance(inverse_root, last_turn)
        advance(empty, last_turn + 1)
        advance(activate, last_turn - 2)
        quantise(later_units[-1])

        for step in range(last_turn, len(jobs) + 2):
            advance(empty, step + 1)
            advance(sums, step + 2)
            if step == last_turn:
                spread_update()
            advance(difference, step)
            advance(mean_of, step + 1)
            advance(statistics, step)
            advance(inverse_root, step)
            advance(centre, step)
            advance(affine, step - 1)
            advance(multiply, step - 2)
            advance(finish, step - 2)
            advance(activate, step - 1)
